import numpy as np
import ml_dtypes


def mxq(x, axis, fmt="e4m3"):
    dtype, down = {"e4m3": (ml_dtypes.float8_e4m3fn, 7), "e5m2": (ml_dtypes.float8_e5m2, 14)}[fmt]
    v = np.moveaxis(np.asarray(x, np.float32).astype(ml_dtypes.bfloat16).astype(np.float64), axis, -1)
    blocks = v.reshape(v.shape[:-1] + (-1, 32))
    amax = np.abs(blocks).max(-1, keepdims=True)
    byte = np.maximum(np.where(amax > 0, np.frexp(amax)[1] - 1 + 127, 0) - down, 1)
    scale = np.exp2(byte - 127.0)
    codes = (blocks / scale).astype(np.float32).astype(dtype).astype(np.float64)
    return np.moveaxis((codes * scale).reshape(v.shape), -1, axis)


WIDE = False


def mx_kscale(k):
    if not WIDE:
        return np.ones(k)
    levels = np.array([10, -10, 5, -5, 0])
    a = np.random.permutation(np.resize(levels, k // 512 * 4)).reshape(k // 512, 4)
    idx = np.arange(k)
    return np.exp2(a[idx // 512, idx % 128 // 32])


BF16 = ml_dtypes.bfloat16


def bf(x):
    return np.asarray(x, np.float32).astype(BF16)


def f64(x):
    return np.asarray(x).astype(np.float64)


E2M1 = np.array([0.0, 0.5, 1.0, 1.5, 2.0, 3.0, 4.0, 6.0, -0.0, -0.5, -1.0, -1.5, -2.0, -3.0, -4.0, -6.0])


def pack_weight(w, fmt):
    k, n = w.shape
    w = f64(bf(w)).reshape(k // 32, 32, n)
    amax = np.abs(w).max(1)
    if fmt == "e4m3":
        byte = np.frexp(amax)[1] - 1 + 127 - 7
    else:
        mant, ex = np.frexp(amax / 6.0)
        byte = np.where(mant > 0.5, ex, ex - 1) + 127
    byte = np.clip(np.where(amax > 0, byte, 1), 1, 254)
    scaled = (w * np.exp2(127.0 - byte)[:, None, :]).reshape(k, n).astype(np.float32)
    by_word = np.ascontiguousarray(scaled.reshape(k // 512, 128, 4, n).transpose(0, 1, 3, 2))
    if fmt == "e4m3":
        words = by_word.astype(ml_dtypes.float8_e4m3fn).view(np.uint8)
    else:
        c = by_word.astype(ml_dtypes.float4_e2m1fn).view(np.uint8) & 0xF
        words = c[..., 0::2] | (c[..., 1::2] << 4)
    return np.ascontiguousarray(words), np.ascontiguousarray(byte.astype(np.uint8).reshape(k // 512, 16, n))


def unpack_weight(words, scales, fmt):
    g, p, n, _ = words.shape
    if fmt == "e4m3":
        vals = np.ascontiguousarray(words).view(ml_dtypes.float8_e4m3fn).astype(np.float64)
    else:
        nib = np.empty((g, p, n, 4), np.uint8)
        nib[..., 0::2] = words & 0xF
        nib[..., 1::2] = words >> 4
        vals = E2M1[nib]
    vals = vals * np.repeat(np.exp2(scales.astype(np.float64) - 127.0), 8, axis=1)[..., None]
    return vals.transpose(0, 1, 3, 2).reshape(g * 512, n)


N, D, N_BRANCH, N_OUT = 2048, 1024, 512, 512
BLOCK = N_BRANCH // 4
FMT = "e4m3"


def erf(v):
    a = np.minimum(np.abs(v), 6.0)
    term = a.copy()
    total = a.copy()
    for n in range(1, 120):
        term = term * (2.0 * a * a) / (2 * n + 1)
        total = total + term
    return np.sign(v) * 2.0 / np.sqrt(np.pi) * np.exp(-a * a) * total


def _branch_activations(h):
    return np.concatenate([
        np.maximum(h[:, 0 * BLOCK:1 * BLOCK], 0.0),
        np.tanh(h[:, 1 * BLOCK:2 * BLOCK]),
        1.0 / (1.0 + np.exp(-h[:, 2 * BLOCK:3 * BLOCK])),
        0.5 * h[:, 3 * BLOCK:4 * BLOCK] * (1.0 + erf(h[:, 3 * BLOCK:4 * BLOCK] / np.sqrt(2.0))),
    ], axis=-1)


def setup_inputs():
    s = mx_kscale(D)
    t = np.ones(N_BRANCH)
    t[:BLOCK] = mx_kscale(N_BRANCH)[:BLOCK]
    x = bf(np.random.standard_normal((N, D)) * s)
    W_words, W_scales = pack_weight(np.random.standard_normal((D, N_BRANCH)) * 1.0 / np.sqrt(D) / s[:, None] * t, FMT)
    b = bf(np.random.standard_normal(N_BRANCH) * 0.3 * t)
    agg_words, agg_scales = pack_weight(np.random.standard_normal((N_BRANCH, N_OUT)) * 1.5 / np.sqrt(N_BRANCH) / t[:, None], FMT)
    return {"x": x,
            "W_words": W_words,
            "W_scales": W_scales,
            "b": b,
            "agg_words": agg_words,
            "agg_scales": agg_scales}


def reference(x, W_words, W_scales, b, agg_words, agg_scales):
    h = (mxq(f64(x), 1, "e4m3") @ unpack_weight(W_words, W_scales, FMT)) + f64(b)
    concatenated = _branch_activations(h)
    return mxq(concatenated, 1, "e4m3") @ unpack_weight(agg_words, agg_scales, FMT)

@@ -1,0 +1,246 @@
+from contextlib import ExitStack
+
+import concourse.mybir as mybir
+from concourse.masks import make_identity
+
+F32 = mybir.dt.float32
+BF16 = mybir.dt.bfloat16
+I32 = mybir.dt.int32
+U32 = mybir.dt.uint32
+U8 = mybir.dt.uint8
+FP8X4 = mybir.dt.float8_e4m3fn_x4
+ACT = mybir.ActivationFunctionType
+ALU = mybir.AluOpType
+
+P = 128
+PACK = 4
+K_PASS = P * PACK
+TOKENS, D_IN, BRANCHES, D_OUT = 2048, 1024, 512, 512
+X_PASSES = D_IN // K_PASS
+TILES = TOKENS // P
+PAIR = 2
+ROUNDS = TILES // PAIR
+QUADRANT = 32
+AGG_PLANE = X_PASSES
+
+FLOPS = 2 * TOKENS * D_IN * BRANCHES + 2 * TOKENS * BRANCHES * D_OUT
+
+
+def tile_kan_kernel(tc, x, W_words, W_scales, b, agg_words, agg_scales, out):
+    nc = tc.nc
+    x_tiles = x.rearrange("(p i) k -> p i k", i=TILES)
+    out_tiles = out.rearrange("(p i) n -> p i n", i=TILES)
+
+    with ExitStack() as stack:
+        consts = stack.enter_context(tc.tile_pool(name="consts", bufs=1))
+        x_pool = stack.enter_context(tc.tile_pool(name="x", bufs=ROUNDS))
+        work = stack.enter_context(tc.tile_pool(name="work", bufs=2))
+        out_pool = stack.enter_context(tc.tile_pool(name="out", bufs=3))
+        psum = stack.enter_context(tc.psum_pool(name="psum", bufs=2))
+        stack.enter_context(tc.manual_schedule())
+
+        planes = consts.tile([P, X_PASSES + 1, BRANCHES], U8, align_bytes=64)
+        nc.vector.memset(planes[:].rearrange("p a n -> p (a n)").bitcast(I32), 0)
+        bias_rows = consts.tile([P, BRANCHES], BF16)
+        nc.vector.memset(bias_rows[:], 0.0)
+        ones = consts.tile([P, P], BF16)
+        nc.vector.memset(ones[:], 1.0)
+        zero_column = consts.tile([P, 1], F32)
+        nc.vector.memset(zero_column[:], 0.0)
+        sigmoid_rows = slice(2 * QUADRANT, 3 * QUADRANT)
+        c_scale = consts.tile([P, 1], F32)
+        nc.vector.memset(c_scale[:], 1.0)
+        nc.vector.memset(c_scale[sigmoid_rows, :], 0.5)
+        c_bias = consts.tile([P, 1], F32)
+        nc.vector.memset(c_bias[:], 0.0)
+        nc.vector.memset(c_bias[sigmoid_rows, :], 0.5)
+        identity = consts.tile([P, P], F32)
+        make_identity(nc, identity[:])
+
+        table_warmer = consts.tile([P, 1], F32)
+        nc.scalar.activation(out=table_warmer[:], in_=zero_column[:], func=ACT.Gelu)
+
+        x_pairs = []
+
+        def load_x(r):
+            x_pair = x_pool.tile([P, PAIR, D_IN], BF16)
+            nc.sync.dma_start(out=x_pair[:], in_=x_tiles[:, PAIR * r : PAIR * (r + 1), :])
+            x_pairs.append(x_pair)
+
+        load_x(0)
+        for quadrant in range(P // QUADRANT):
+            live = slice(QUADRANT * quadrant, QUADRANT * quadrant + PACK)
+            rows = slice(PACK * quadrant, PACK * (quadrant + 1))
+            nc.sync.dma_start(
+                out=planes[live, 0:X_PASSES, :].bitcast(I32),
+                in_=W_scales[:, rows, :].rearrange("g q n -> q g n").bitcast(I32),
+            )
+        w_words = consts.tile([P, X_PASSES, PACK * BRANCHES], U8, align_bytes=64)
+        nc.sync.dma_start(
+            out=w_words[:].bitcast(I32),
+            in_=W_words.rearrange("g p n t -> p g (n t)").bitcast(I32),
+        )
+        nc.sync.dma_start(out=bias_rows[0:1, :], in_=b.unsqueeze(0))
+        load_x(1)
+        for quadrant in range(P // QUADRANT):
+            live = slice(QUADRANT * quadrant, QUADRANT * quadrant + PACK)
+            rows = slice(PACK * quadrant, PACK * (quadrant + 1))
+            nc.sync.dma_start(
+                out=planes[live, AGG_PLANE, :].bitcast(I32),
+                in_=agg_scales[0, rows, :].bitcast(I32),
+            )
+        a_words = consts.tile([P, PACK * D_OUT], U8, align_bytes=64)
+        nc.sync.dma_start(
+            out=a_words[:].bitcast(I32),
+            in_=agg_words[0].rearrange("p n t -> p (n t)").bitcast(I32),
+        )
+        for r in range(2, ROUNDS):
+            load_x(r)
+
+        bias_sorted = consts.tile([P, PACK, P], F32)
+
+        def spread_bias():
+            bias_bank = psum.tile([P, BRANCHES], F32, tag="h")
+            nc.tensor.matmul(
+                out=bias_bank[:], lhsT=ones[:], rhs=bias_rows[:], start=True, stop=True
+            )
+            nc.vector.tensor_copy(
+                out=bias_sorted[:], in_=bias_bank[:].rearrange("p (w s) -> p s w", s=PACK)
+            )
+
+        x_grouped_of, x_mx_of, h_of, act_of, c_grouped_of, c_mx_of, o_of = {}, {}, {}, {}, {}, {}, {}
+
+        def transpose_x(r):
+            x_grouped = work.tile([P, PAIR, X_PASSES, P, PACK], BF16, align_bytes=64)
+            for j in range(PAIR):
+                x_f32 = x_pairs[r][:, j, :].bitcast(F32)
+                xt = psum.tile([P, X_PASSES, 2, P], F32, tag="xt")
+                for g in range(X_PASSES):
+                    first = g * K_PASS // 2
+                    for u in range(2):
+                        nc.tensor.transpose(
+                            xt[:, g, u, :], x_f32[:, first + u : first + K_PASS // 2 : 2], identity[:]
+                        )
+                nc.vector.tensor_copy(
+                    out=x_grouped[:, j]
+                    .rearrange("p g t s -> p (g t s)")
+                    .bitcast(F32)
+                    .rearrange("p (g t u) -> p g t u", g=X_PASSES, u=2),
+                    in_=xt[:].rearrange("p g u t -> p g t u"),
+                )
+            x_grouped_of[r] = x_grouped
+
+        def quantise_x(r):
+            x_codes = work.tile([P, PAIR, X_PASSES, P], U32, align_bytes=64)
+            x_scales = work.tile([P, PAIR, X_PASSES, P], U8, align_bytes=64)
+            nc.vector.quantize_mx(
+                out=x_codes[:].rearrange("p j g t -> p (j g t)").bitcast(FP8X4),
+                scales=x_scales[:].rearrange("p j g t -> p (j g t)"),
+                in_=x_grouped_of[r][:].rearrange("p j g t s -> p (j g t s)"),
+            )
+            x_mx_of[r] = (x_codes, x_scales)
+
+        def first_product(r):
+            x_codes, x_scales = x_mx_of[r]
+            h_of[r] = []
+            for j in range(PAIR):
+                h = psum.tile([P, BRANCHES], F32, tag="h")
+                for g in range(X_PASSES):
+                    nc.tensor.matmul_mx(
+                        out=h[:],
+                        lhsT=x_codes[:, j, g, :].bitcast(FP8X4),
+                        lhsT_scale=x_scales[:, j, g, :],
+                        rhs=w_words[:, g, :].bitcast(FP8X4),
+                        rhs_scale=planes[:, g, :],
+                        start=(g == 0),
+                        stop=(g == X_PASSES - 1),
+                    )
+                h_of[r].append(h)
+
+        def activate(r):
+            biased = work.tile([P, PAIR, PACK, P], F32)
+            for j in range(PAIR):
+                nc.vector.tensor_tensor(
+                    out=biased[:, j],
+                    in0=h_of[r][j][:].rearrange("p (w s) -> p s w", s=PACK),
+                    in1=bias_sorted[:],
+                    op=ALU.add,
+                )
+            activated = work.tile([P, PAIR, PACK, P], F32)
+            functions = ((ACT.Relu, 1.0), (ACT.Tanh, 1.0), (ACT.Tanh, 0.5), (ACT.Gelu, 1.0))
+            for block, (func, scale) in enumerate(functions):
+                cols = slice(QUADRANT * block, QUADRANT * (block + 1))
+                nc.scalar.activation(
+                    out=activated[:, :, :, cols], in_=biased[:, :, :, cols], func=func, scale=scale
+                )
+            act_of[r] = activated
+
+        def transpose_c(r):
+            c_grouped = work.tile([P, PAIR, P, PACK], BF16, align_bytes=64)
+            for j in range(PAIR):
+                ct = psum.tile([P, PACK, P], F32, tag="ct")
+                for s in range(PACK):
+                    nc.tensor.transpose(ct[:, s, :], act_of[r][:, j, s, :], identity[:])
+                nc.scalar.activation(
+                    out=c_grouped[:, j],
+                    in_=ct[:].rearrange("p s t -> p t s"),
+                    func=ACT.Identity,
+                    scale=c_scale[:, 0:1],
+                    bias=c_bias[:, 0:1],
+                )
+            c_grouped_of[r] = c_grouped
+
+        def quantise_c(r):
+            c_codes = work.tile([P, PAIR, P], U32, align_bytes=64)
+            c_scales = work.tile([P, PAIR, P], U8, align_bytes=64)
+            nc.vector.quantize_mx(
+                out=c_codes[:].rearrange("p j t -> p (j t)").bitcast(FP8X4),
+                scales=c_scales[:].rearrange("p j t -> p (j t)"),
+                in_=c_grouped_of[r][:].rearrange("p j t s -> p (j t s)"),
+            )
+            c_mx_of[r] = (c_codes, c_scales)
+
+        def second_product(r):
+            c_codes, c_scales = c_mx_of[r]
+            o_of[r] = []
+            for j in range(PAIR):
+                o = psum.tile([P, D_OUT], F32, tag="o")
+                nc.tensor.matmul_mx(
+                    out=o[:],
+                    lhsT=c_codes[:, j, :].bitcast(FP8X4),
+                    lhsT_scale=c_scales[:, j, :],
+                    rhs=a_words[:].bitcast(FP8X4),
+                    rhs_scale=planes[:, AGG_PLANE, :],
+                    start=True,
+                    stop=True,
+                )
+                o_of[r].append(o)
+
+        def store(r):
+            result = out_pool.tile([P, PAIR, D_OUT], F32)
+            for j in range(PAIR):
+                nc.scalar.copy(out=result[:, j, :], in_=o_of[r][j][:])
+            nc.sync.dma_start(out=out_tiles[:, PAIR * r : PAIR * (r + 1), :], in_=result[:])
+
+        def in_range(pair):
+            return 0 <= pair < ROUNDS
+
+        for r in range(ROUNDS + 5):
+            if in_range(r - 1):
+                quantise_x(r - 1)
+            if in_range(r - 4):
+                quantise_c(r - 4)
+            if in_range(r - 5):
+                store(r - 5)
+            if in_range(r - 2):
+                activate(r - 2)
+            if in_range(r):
+                transpose_x(r)
+            if r == 0:
+                spread_bias()
+            if in_range(r - 3):
+                transpose_c(r - 3)
+            if in_range(r - 1):
+                first_product(r - 1)
+            if in_range(r - 4):
+                second_product(r - 4)

@@ -35,7 +35,7 @@ def tile_kan_kernel(tc, x, W_words, W_scales, b, agg_words, agg_scales, out):
         consts = stack.enter_context(tc.tile_pool(name="consts", bufs=1))
         x_pool = stack.enter_context(tc.tile_pool(name="x", bufs=ROUNDS))
         work = stack.enter_context(tc.tile_pool(name="work", bufs=2))
-        out_pool = stack.enter_context(tc.tile_pool(name="out", bufs=3))
+        out_pool = stack.enter_context(tc.tile_pool(name="out", bufs=4))
         psum = stack.enter_context(tc.psum_pool(name="psum", bufs=2))
         stack.enter_context(tc.manual_schedule())
 
@@ -64,7 +64,8 @@ def tile_kan_kernel(tc, x, W_words, W_scales, b, agg_words, agg_scales, out):
 
         def load_x(r):
             x_pair = x_pool.tile([P, PAIR, D_IN], BF16)
-            nc.sync.dma_start(out=x_pair[:], in_=x_tiles[:, PAIR * r : PAIR * (r + 1), :])
+            for j in range(PAIR):
+                nc.sync.dma_start(out=x_pair[:, j, :], in_=x_tiles[:, PAIR * r + j, :])
             x_pairs.append(x_pair)
 
         load_x(0)
@@ -108,7 +109,8 @@ def tile_kan_kernel(tc, x, W_words, W_scales, b, agg_words, agg_scales, out):
                 out=bias_sorted[:], in_=bias_bank[:].rearrange("p (w s) -> p s w", s=PACK)
             )
 
-        x_grouped_of, x_mx_of, h_of, act_of, c_grouped_of, c_mx_of, o_of = {}, {}, {}, {}, {}, {}, {}
+        x_grouped_of, x_mx_of, h_of, biased_of = {}, {}, {}, {}
+        act_of, c_grouped_of, c_mx_of, o_of = {}, {}, {}, {}
 
         def transpose_x(r):
             x_grouped = work.tile([P, PAIR, X_PASSES, P, PACK], BF16, align_bytes=64)
@@ -121,7 +123,7 @@ def tile_kan_kernel(tc, x, W_words, W_scales, b, agg_words, agg_scales, out):
                         nc.tensor.transpose(
                             xt[:, g, u, :], x_f32[:, first + u : first + K_PASS // 2 : 2], identity[:]
                         )
-                nc.vector.tensor_copy(
+                nc.scalar.copy(
                     out=x_grouped[:, j]
                     .rearrange("p g t s -> p (g t s)")
                     .bitcast(F32)
@@ -157,7 +159,7 @@ def tile_kan_kernel(tc, x, W_words, W_scales, b, agg_words, agg_scales, out):
                     )
                 h_of[r].append(h)
 
-        def activate(r):
+        def add_bias(r):
             biased = work.tile([P, PAIR, PACK, P], F32)
             for j in range(PAIR):
                 nc.vector.tensor_tensor(
@@ -167,13 +169,22 @@ def tile_kan_kernel(tc, x, W_words, W_scales, b, agg_words, agg_scales, out):
                     op=ALU.add,
                 )
             activated = work.tile([P, PAIR, PACK, P], F32)
-            functions = ((ACT.Relu, 1.0), (ACT.Tanh, 1.0), (ACT.Tanh, 0.5), (ACT.Gelu, 1.0))
-            for block, (func, scale) in enumerate(functions):
+            nc.vector.tensor_scalar_max(
+                out=activated[:, :, :, 0:QUADRANT], in0=biased[:, :, :, 0:QUADRANT], scalar1=0.0
+            )
+            biased_of[r] = biased
+            act_of[r] = activated
+
+        def activate(r):
+            functions = ((ACT.Tanh, 1.0), (ACT.Tanh, 0.5), (ACT.Gelu, 1.0))
+            for block, (func, scale) in enumerate(functions, start=1):
                 cols = slice(QUADRANT * block, QUADRANT * (block + 1))
                 nc.scalar.activation(
-                    out=activated[:, :, :, cols], in_=biased[:, :, :, cols], func=func, scale=scale
+                    out=act_of[r][:, :, :, cols],
+                    in_=biased_of[r][:, :, :, cols],
+                    func=func,
+                    scale=scale,
                 )
-            act_of[r] = activated
 
         def transpose_c(r):
             c_grouped = work.tile([P, PAIR, P, PACK], BF16, align_bytes=64)
@@ -217,10 +228,10 @@ def tile_kan_kernel(tc, x, W_words, W_scales, b, agg_words, agg_scales, out):
                 o_of[r].append(o)
 
         def store(r):
-            result = out_pool.tile([P, PAIR, D_OUT], F32)
             for j in range(PAIR):
-                nc.scalar.copy(out=result[:, j, :], in_=o_of[r][j][:])
-            nc.sync.dma_start(out=out_tiles[:, PAIR * r : PAIR * (r + 1), :], in_=result[:])
+                result = out_pool.tile([P, D_OUT], F32)
+                nc.vector.tensor_copy(out=result[:], in_=o_of[r][j][:])
+                nc.sync.dma_start(out=out_tiles[:, PAIR * r + j, :], in_=result[:])
 
         def in_range(pair):
             return 0 <= pair < ROUNDS
@@ -230,16 +241,18 @@ def tile_kan_kernel(tc, x, W_words, W_scales, b, agg_words, agg_scales, out):
                 quantise_x(r - 1)
             if in_range(r - 4):
                 quantise_c(r - 4)
+            if in_range(r - 2):
+                add_bias(r - 2)
             if in_range(r - 5):
                 store(r - 5)
-            if in_range(r - 2):
-                activate(r - 2)
             if in_range(r):
                 transpose_x(r)
             if r == 0:
                 spread_bias()
             if in_range(r - 3):
                 transpose_c(r - 3)
+            if in_range(r - 2):
+                activate(r - 2)
             if in_range(r - 1):
                 first_product(r - 1)
             if in_range(r - 4):

@@ -18,8 +18,8 @@ K_PASS = P * PACK
 TOKENS, D_IN, BRANCHES, D_OUT = 2048, 1024, 512, 512
 X_PASSES = D_IN // K_PASS
 TILES = TOKENS // P
-PAIR = 2
-ROUNDS = TILES // PAIR
+BATCH = 1
+ROUNDS = TILES // BATCH
 QUADRANT = 32
 AGG_PLANE = X_PASSES
 
@@ -60,13 +60,13 @@ def tile_kan_kernel(tc, x, W_words, W_scales, b, agg_words, agg_scales, out):
         table_warmer = consts.tile([P, 1], F32)
         nc.scalar.activation(out=table_warmer[:], in_=zero_column[:], func=ACT.Gelu)
 
-        x_pairs = []
+        x_batches = []
 
         def load_x(r):
-            x_pair = x_pool.tile([P, PAIR, D_IN], BF16)
-            for j in range(PAIR):
-                nc.sync.dma_start(out=x_pair[:, j, :], in_=x_tiles[:, PAIR * r + j, :])
-            x_pairs.append(x_pair)
+            x_batch = x_pool.tile([P, BATCH, D_IN], BF16)
+            for j in range(BATCH):
+                nc.sync.dma_start(out=x_batch[:, j, :], in_=x_tiles[:, BATCH * r + j, :])
+            x_batches.append(x_batch)
 
         load_x(0)
         for quadrant in range(P // QUADRANT):
@@ -113,9 +113,9 @@ def tile_kan_kernel(tc, x, W_words, W_scales, b, agg_words, agg_scales, out):
         act_of, c_grouped_of, c_mx_of, o_of = {}, {}, {}, {}
 
         def transpose_x(r):
-            x_grouped = work.tile([P, PAIR, X_PASSES, P, PACK], BF16, align_bytes=64)
-            for j in range(PAIR):
-                x_f32 = x_pairs[r][:, j, :].bitcast(F32)
+            x_grouped = work.tile([P, BATCH, X_PASSES, P, PACK], BF16, align_bytes=64)
+            for j in range(BATCH):
+                x_f32 = x_batches[r][:, j, :].bitcast(F32)
                 xt = psum.tile([P, X_PASSES, 2, P], F32, tag="xt")
                 for g in range(X_PASSES):
                     first = g * K_PASS // 2
@@ -133,8 +133,8 @@ def tile_kan_kernel(tc, x, W_words, W_scales, b, agg_words, agg_scales, out):
             x_grouped_of[r] = x_grouped
 
         def quantise_x(r):
-            x_codes = work.tile([P, PAIR, X_PASSES, P], U32, align_bytes=64)
-            x_scales = work.tile([P, PAIR, X_PASSES, P], U8, align_bytes=64)
+            x_codes = work.tile([P, BATCH, X_PASSES, P], U32, align_bytes=64)
+            x_scales = work.tile([P, BATCH, X_PASSES, P], U8, align_bytes=64)
             nc.vector.quantize_mx(
                 out=x_codes[:].rearrange("p j g t -> p (j g t)").bitcast(FP8X4),
                 scales=x_scales[:].rearrange("p j g t -> p (j g t)"),
@@ -145,7 +145,7 @@ def tile_kan_kernel(tc, x, W_words, W_scales, b, agg_words, agg_scales, out):
         def first_product(r):
             x_codes, x_scales = x_mx_of[r]
             h_of[r] = []
-            for j in range(PAIR):
+            for j in range(BATCH):
                 h = psum.tile([P, BRANCHES], F32, tag="h")
                 for g in range(X_PASSES):
                     nc.tensor.matmul_mx(
@@ -160,15 +160,15 @@ def tile_kan_kernel(tc, x, W_words, W_scales, b, agg_words, agg_scales, out):
                 h_of[r].append(h)
 
         def add_bias(r):
-            biased = work.tile([P, PAIR, PACK, P], F32)
-            for j in range(PAIR):
+            biased = work.tile([P, BATCH, PACK, P], F32)
+            for j in range(BATCH):
                 nc.vector.tensor_tensor(
                     out=biased[:, j],
                     in0=h_of[r][j][:].rearrange("p (w s) -> p s w", s=PACK),
                     in1=bias_sorted[:],
                     op=ALU.add,
                 )
-            activated = work.tile([P, PAIR, PACK, P], F32)
+            activated = work.tile([P, BATCH, PACK, P], F32)
             nc.vector.tensor_scalar_max(
                 out=activated[:, :, :, 0:QUADRANT], in0=biased[:, :, :, 0:QUADRANT], scalar1=0.0
             )
@@ -187,8 +187,8 @@ def tile_kan_kernel(tc, x, W_words, W_scales, b, agg_words, agg_scales, out):
                 )
 
         def transpose_c(r):
-            c_grouped = work.tile([P, PAIR, P, PACK], BF16, align_bytes=64)
-            for j in range(PAIR):
+            c_grouped = work.tile([P, BATCH, P, PACK], BF16, align_bytes=64)
+            for j in range(BATCH):
                 ct = psum.tile([P, PACK, P], F32, tag="ct")
                 for s in range(PACK):
                     nc.tensor.transpose(ct[:, s, :], act_of[r][:, j, s, :], identity[:])
@@ -202,8 +202,8 @@ def tile_kan_kernel(tc, x, W_words, W_scales, b, agg_words, agg_scales, out):
             c_grouped_of[r] = c_grouped
 
         def quantise_c(r):
-            c_codes = work.tile([P, PAIR, P], U32, align_bytes=64)
-            c_scales = work.tile([P, PAIR, P], U8, align_bytes=64)
+            c_codes = work.tile([P, BATCH, P], U32, align_bytes=64)
+            c_scales = work.tile([P, BATCH, P], U8, align_bytes=64)
             nc.vector.quantize_mx(
                 out=c_codes[:].rearrange("p j t -> p (j t)").bitcast(FP8X4),
                 scales=c_scales[:].rearrange("p j t -> p (j t)"),
@@ -214,7 +214,7 @@ def tile_kan_kernel(tc, x, W_words, W_scales, b, agg_words, agg_scales, out):
         def second_product(r):
             c_codes, c_scales = c_mx_of[r]
             o_of[r] = []
-            for j in range(PAIR):
+            for j in range(BATCH):
                 o = psum.tile([P, D_OUT], F32, tag="o")
                 nc.tensor.matmul_mx(
                     out=o[:],
@@ -228,13 +228,13 @@ def tile_kan_kernel(tc, x, W_words, W_scales, b, agg_words, agg_scales, out):
                 o_of[r].append(o)
 
         def store(r):
-            for j in range(PAIR):
+            for j in range(BATCH):
                 result = out_pool.tile([P, D_OUT], F32)
                 nc.vector.tensor_copy(out=result[:], in_=o_of[r][j][:])
-                nc.sync.dma_start(out=out_tiles[:, PAIR * r + j, :], in_=result[:])
+                nc.sync.dma_start(out=out_tiles[:, BATCH * r + j, :], in_=result[:])
 
-        def in_range(pair):
-            return 0 <= pair < ROUNDS
+        def in_range(batch):
+            return 0 <= batch < ROUNDS
 
         for r in range(ROUNDS + 5):
             if in_range(r - 1):

@@ -18,7 +18,7 @@ K_PASS = P * PACK
 TOKENS, D_IN, BRANCHES, D_OUT = 2048, 1024, 512, 512
 X_PASSES = D_IN // K_PASS
 TILES = TOKENS // P
-BATCH = 1
+BATCH = 2
 ROUNDS = TILES // BATCH
 QUADRANT = 32
 AGG_PLANE = X_PASSES
@@ -36,7 +36,8 @@ def tile_kan_kernel(tc, x, W_words, W_scales, b, agg_words, agg_scales, out):
         x_pool = stack.enter_context(tc.tile_pool(name="x", bufs=ROUNDS))
         work = stack.enter_context(tc.tile_pool(name="work", bufs=2))
         out_pool = stack.enter_context(tc.tile_pool(name="out", bufs=4))
-        psum = stack.enter_context(tc.psum_pool(name="psum", bufs=2))
+        psum_transposes = stack.enter_context(tc.psum_pool(name="psum_transposes", bufs=4))
+        psum_products = stack.enter_context(tc.psum_pool(name="psum_products", bufs=4))
         stack.enter_context(tc.manual_schedule())
 
         planes = consts.tile([P, X_PASSES + 1, BRANCHES], U8, align_bytes=64)
@@ -69,6 +70,7 @@ def tile_kan_kernel(tc, x, W_words, W_scales, b, agg_words, agg_scales, out):
             x_batches.append(x_batch)
 
         load_x(0)
+        load_x(1)
         for quadrant in range(P // QUADRANT):
             live = slice(QUADRANT * quadrant, QUADRANT * quadrant + PACK)
             rows = slice(PACK * quadrant, PACK * (quadrant + 1))
@@ -82,7 +84,8 @@ def tile_kan_kernel(tc, x, W_words, W_scales, b, agg_words, agg_scales, out):
             in_=W_words.rearrange("g p n t -> p g (n t)").bitcast(I32),
         )
         nc.sync.dma_start(out=bias_rows[0:1, :], in_=b.unsqueeze(0))
-        load_x(1)
+        load_x(2)
+        load_x(3)
         for quadrant in range(P // QUADRANT):
             live = slice(QUADRANT * quadrant, QUADRANT * quadrant + PACK)
             rows = slice(PACK * quadrant, PACK * (quadrant + 1))
@@ -95,13 +98,13 @@ def tile_kan_kernel(tc, x, W_words, W_scales, b, agg_words, agg_scales, out):
             out=a_words[:].bitcast(I32),
             in_=agg_words[0].rearrange("p n t -> p (n t)").bitcast(I32),
         )
-        for r in range(2, ROUNDS):
+        for r in range(4, ROUNDS):
             load_x(r)
 
         bias_sorted = consts.tile([P, PACK, P], F32)
 
         def spread_bias():
-            bias_bank = psum.tile([P, BRANCHES], F32, tag="h")
+            bias_bank = psum_products.tile([P, BRANCHES], F32, tag="product")
             nc.tensor.matmul(
                 out=bias_bank[:], lhsT=ones[:], rhs=bias_rows[:], start=True, stop=True
             )
@@ -109,21 +112,28 @@ def tile_kan_kernel(tc, x, W_words, W_scales, b, agg_words, agg_scales, out):
                 out=bias_sorted[:], in_=bias_bank[:].rearrange("p (w s) -> p s w", s=PACK)
             )
 
+        def copy_out_of_psum(j, out, in_):
+            if j % 2 == 0:
+                nc.scalar.copy(out=out, in_=in_)
+            else:
+                nc.vector.tensor_copy(out=out, in_=in_)
+
         x_grouped_of, x_mx_of, h_of, biased_of = {}, {}, {}, {}
-        act_of, c_grouped_of, c_mx_of, o_of = {}, {}, {}, {}
+        act_of, ct_of, c_grouped_of, c_mx_of, o_of = {}, {}, {}, {}, {}
 
         def transpose_x(r):
             x_grouped = work.tile([P, BATCH, X_PASSES, P, PACK], BF16, align_bytes=64)
             for j in range(BATCH):
                 x_f32 = x_batches[r][:, j, :].bitcast(F32)
-                xt = psum.tile([P, X_PASSES, 2, P], F32, tag="xt")
+                xt = psum_transposes.tile([P, X_PASSES, 2, P], F32, tag="transposed")
                 for g in range(X_PASSES):
                     first = g * K_PASS // 2
                     for u in range(2):
                         nc.tensor.transpose(
                             xt[:, g, u, :], x_f32[:, first + u : first + K_PASS // 2 : 2], identity[:]
                         )
-                nc.scalar.copy(
+                copy_out_of_psum(
+                    j,
                     out=x_grouped[:, j]
                     .rearrange("p g t s -> p (g t s)")
                     .bitcast(F32)
@@ -146,7 +156,7 @@ def tile_kan_kernel(tc, x, W_words, W_scales, b, agg_words, agg_scales, out):
             x_codes, x_scales = x_mx_of[r]
             h_of[r] = []
             for j in range(BATCH):
-                h = psum.tile([P, BRANCHES], F32, tag="h")
+                h = psum_products.tile([P, BRANCHES], F32, tag="product")
                 for g in range(X_PASSES):
                     nc.tensor.matmul_mx(
                         out=h[:],
@@ -168,11 +178,15 @@ def tile_kan_kernel(tc, x, W_words, W_scales, b, agg_words, agg_scales, out):
                     in1=bias_sorted[:],
                     op=ALU.add,
                 )
+            biased_of[r] = biased
+
+        def relu(r):
             activated = work.tile([P, BATCH, PACK, P], F32)
             nc.vector.tensor_scalar_max(
-                out=activated[:, :, :, 0:QUADRANT], in0=biased[:, :, :, 0:QUADRANT], scalar1=0.0
+                out=activated[:, :, :, 0:QUADRANT],
+                in0=biased_of[r][:, :, :, 0:QUADRANT],
+                scalar1=0.0,
             )
-            biased_of[r] = biased
             act_of[r] = activated
 
         def activate(r):
@@ -187,14 +201,19 @@ def tile_kan_kernel(tc, x, W_words, W_scales, b, agg_words, agg_scales, out):
                 )
 
         def transpose_c(r):
-            c_grouped = work.tile([P, BATCH, P, PACK], BF16, align_bytes=64)
+            ct_of[r] = []
             for j in range(BATCH):
-                ct = psum.tile([P, PACK, P], F32, tag="ct")
+                ct = psum_transposes.tile([P, PACK, P], F32, tag="transposed")
                 for s in range(PACK):
                     nc.tensor.transpose(ct[:, s, :], act_of[r][:, j, s, :], identity[:])
+                ct_of[r].append(ct)
+
+        def group_c(r):
+            c_grouped = work.tile([P, BATCH, P, PACK], BF16, align_bytes=64)
+            for j in range(BATCH):
                 nc.scalar.activation(
                     out=c_grouped[:, j],
-                    in_=ct[:].rearrange("p s t -> p t s"),
+                    in_=ct_of[r][j][:].rearrange("p s t -> p t s"),
                     func=ACT.Identity,
                     scale=c_scale[:, 0:1],
                     bias=c_bias[:, 0:1],
@@ -215,7 +234,7 @@ def tile_kan_kernel(tc, x, W_words, W_scales, b, agg_words, agg_scales, out):
             c_codes, c_scales = c_mx_of[r]
             o_of[r] = []
             for j in range(BATCH):
-                o = psum.tile([P, D_OUT], F32, tag="o")
+                o = psum_products.tile([P, D_OUT], F32, tag="product")
                 nc.tensor.matmul_mx(
                     out=o[:],
                     lhsT=c_codes[:, j, :].bitcast(FP8X4),
@@ -230,7 +249,7 @@ def tile_kan_kernel(tc, x, W_words, W_scales, b, agg_words, agg_scales, out):
         def store(r):
             for j in range(BATCH):
                 result = out_pool.tile([P, D_OUT], F32)
-                nc.vector.tensor_copy(out=result[:], in_=o_of[r][j][:])
+                copy_out_of_psum(j, out=result[:], in_=o_of[r][j][:])
                 nc.sync.dma_start(out=out_tiles[:, BATCH * r + j, :], in_=result[:])
 
         def in_range(batch):
@@ -239,20 +258,24 @@ def tile_kan_kernel(tc, x, W_words, W_scales, b, agg_words, agg_scales, out):
         for r in range(ROUNDS + 5):
             if in_range(r - 1):
                 quantise_x(r - 1)
-            if in_range(r - 4):
-                quantise_c(r - 4)
             if in_range(r - 2):
                 add_bias(r - 2)
+            if in_range(r - 4):
+                quantise_c(r - 4)
             if in_range(r - 5):
                 store(r - 5)
+            if in_range(r - 2):
+                relu(r - 2)
             if in_range(r):
                 transpose_x(r)
-            if r == 0:
+            if r == 1:
                 spread_bias()
             if in_range(r - 3):
                 transpose_c(r - 3)
             if in_range(r - 2):
                 activate(r - 2)
+            if in_range(r - 3):
+                group_c(r - 3)
             if in_range(r - 1):
                 first_product(r - 1)
             if in_range(r - 4):

@@ -10,18 +10,20 @@ U32 = mybir.dt.uint32
 U8 = mybir.dt.uint8
 FP8X4 = mybir.dt.float8_e4m3fn_x4
 ACT = mybir.ActivationFunctionType
-ALU = mybir.AluOpType
 
 P = 128
 PACK = 4
 K_PASS = P * PACK
 TOKENS, D_IN, BRANCHES, D_OUT = 2048, 1024, 512, 512
 X_PASSES = D_IN // K_PASS
+FUNCTIONS = BRANCHES // P
 TILES = TOKENS // P
 BATCH = 2
+BATCH_TOKENS = BATCH * P
 ROUNDS = TILES // BATCH
-QUADRANT = 32
+WORD_ROWS = P // PACK
 AGG_PLANE = X_PASSES
+LOADS_AHEAD = 4
 
 FLOPS = 2 * TOKENS * D_IN * BRANCHES + 2 * TOKENS * BRANCHES * D_OUT
 
@@ -35,26 +37,19 @@ def tile_kan_kernel(tc, x, W_words, W_scales, b, agg_words, agg_scales, out):
         consts = stack.enter_context(tc.tile_pool(name="consts", bufs=1))
         x_pool = stack.enter_context(tc.tile_pool(name="x", bufs=ROUNDS))
         work = stack.enter_context(tc.tile_pool(name="work", bufs=2))
-        out_pool = stack.enter_context(tc.tile_pool(name="out", bufs=4))
+        moved = stack.enter_context(tc.tile_pool(name="moved", bufs=4))
         psum_transposes = stack.enter_context(tc.psum_pool(name="psum_transposes", bufs=4))
         psum_products = stack.enter_context(tc.psum_pool(name="psum_products", bufs=4))
         stack.enter_context(tc.manual_schedule())
 
         planes = consts.tile([P, X_PASSES + 1, BRANCHES], U8, align_bytes=64)
         nc.vector.memset(planes[:].rearrange("p a n -> p (a n)").bitcast(I32), 0)
-        bias_rows = consts.tile([P, BRANCHES], BF16)
+        bias_rows = consts.tile([P, P], F32)
         nc.vector.memset(bias_rows[:], 0.0)
-        ones = consts.tile([P, P], BF16)
-        nc.vector.memset(ones[:], 1.0)
         zero_column = consts.tile([P, 1], F32)
         nc.vector.memset(zero_column[:], 0.0)
-        sigmoid_rows = slice(2 * QUADRANT, 3 * QUADRANT)
-        c_scale = consts.tile([P, 1], F32)
-        nc.vector.memset(c_scale[:], 1.0)
-        nc.vector.memset(c_scale[sigmoid_rows, :], 0.5)
-        c_bias = consts.tile([P, 1], F32)
-        nc.vector.memset(c_bias[:], 0.0)
-        nc.vector.memset(c_bias[sigmoid_rows, :], 0.5)
+        half_column = consts.tile([P, 1], F32)
+        nc.vector.memset(half_column[:], 0.5)
         identity = consts.tile([P, P], F32)
         make_identity(nc, identity[:])
 
@@ -65,51 +60,47 @@ def tile_kan_kernel(tc, x, W_words, W_scales, b, agg_words, agg_scales, out):
 
         def load_x(r):
             x_batch = x_pool.tile([P, BATCH, D_IN], BF16)
-            for j in range(BATCH):
-                nc.sync.dma_start(out=x_batch[:, j, :], in_=x_tiles[:, BATCH * r + j, :])
+            nc.sync.dma_start(out=x_batch[:], in_=x_tiles[:, BATCH * r : BATCH * (r + 1), :])
             x_batches.append(x_batch)
+
+        def load_scales(plane_slots, scale_rows):
+            for quadrant in range(PACK):
+                nc.sync.dma_start(
+                    out=planes[32 * quadrant : 32 * quadrant + PACK, plane_slots, :].bitcast(I32),
+                    in_=scale_rows[:, PACK * quadrant : PACK * (quadrant + 1), :]
+                    .rearrange("g q n -> q g n")
+                    .bitcast(I32),
+                )
 
         load_x(0)
         load_x(1)
-        for quadrant in range(P // QUADRANT):
-            live = slice(QUADRANT * quadrant, QUADRANT * quadrant + PACK)
-            rows = slice(PACK * quadrant, PACK * (quadrant + 1))
-            nc.sync.dma_start(
-                out=planes[live, 0:X_PASSES, :].bitcast(I32),
-                in_=W_scales[:, rows, :].rearrange("g q n -> q g n").bitcast(I32),
-            )
+        load_scales(slice(0, X_PASSES), W_scales)
         w_words = consts.tile([P, X_PASSES, PACK * BRANCHES], U8, align_bytes=64)
         nc.sync.dma_start(
             out=w_words[:].bitcast(I32),
             in_=W_words.rearrange("g p n t -> p g (n t)").bitcast(I32),
         )
-        nc.sync.dma_start(out=bias_rows[0:1, :], in_=b.unsqueeze(0))
-        load_x(2)
-        load_x(3)
-        for quadrant in range(P // QUADRANT):
-            live = slice(QUADRANT * quadrant, QUADRANT * quadrant + PACK)
-            rows = slice(PACK * quadrant, PACK * (quadrant + 1))
-            nc.sync.dma_start(
-                out=planes[live, AGG_PLANE, :].bitcast(I32),
-                in_=agg_scales[0, rows, :].bitcast(I32),
-            )
+        bias_stage = consts.tile([FUNCTIONS, P], BF16)
+        nc.sync.dma_start(out=bias_stage[:], in_=b.rearrange("(f m) -> f m", f=FUNCTIONS))
+        for r in range(2, LOADS_AHEAD):
+            load_x(r)
+        load_scales(slice(AGG_PLANE, AGG_PLANE + 1), agg_scales)
         a_words = consts.tile([P, PACK * D_OUT], U8, align_bytes=64)
         nc.sync.dma_start(
             out=a_words[:].bitcast(I32),
             in_=agg_words[0].rearrange("p n t -> p (n t)").bitcast(I32),
         )
-        for r in range(4, ROUNDS):
-            load_x(r)
 
-        bias_sorted = consts.tile([P, PACK, P], F32)
+        bias_columns = consts.tile([P, FUNCTIONS], F32)
+        half_sigmoid_bias = consts.tile([P, 1], F32)
 
-        def spread_bias():
-            bias_bank = psum_products.tile([P, BRANCHES], F32, tag="product")
-            nc.tensor.matmul(
-                out=bias_bank[:], lhsT=ones[:], rhs=bias_rows[:], start=True, stop=True
-            )
-            nc.vector.tensor_copy(
-                out=bias_sorted[:], in_=bias_bank[:].rearrange("p (w s) -> p s w", s=PACK)
+        def turn_bias():
+            nc.vector.tensor_copy(out=bias_rows[0:FUNCTIONS, :], in_=bias_stage[:])
+            bias_bank = psum_transposes.tile([P, P], F32, tag="transposed")
+            nc.tensor.transpose(bias_bank[:], bias_rows[:], identity[:])
+            nc.vector.tensor_copy(out=bias_columns[:], in_=bias_bank[:, 0:FUNCTIONS])
+            nc.vector.tensor_scalar_mul(
+                out=half_sigmoid_bias[:], in0=bias_columns[:, 2:3], scalar1=0.5
             )
 
         def copy_out_of_psum(j, out, in_):
@@ -118,11 +109,10 @@ def tile_kan_kernel(tc, x, W_words, W_scales, b, agg_words, agg_scales, out):
             else:
                 nc.vector.tensor_copy(out=out, in_=in_)
 
-        x_grouped_of, x_mx_of, h_of, biased_of = {}, {}, {}, {}
-        act_of, ct_of, c_grouped_of, c_mx_of, o_of = {}, {}, {}, {}, {}
+        x_grouped_of, x_mx_of, h_of, planar_of, c_grouped_of, c_mx_of, o_of = {}, {}, {}, {}, {}, {}, {}
 
         def transpose_x(r):
-            x_grouped = work.tile([P, BATCH, X_PASSES, P, PACK], BF16, align_bytes=64)
+            x_grouped = work.tile([P, X_PASSES, BATCH, P, PACK], BF16, align_bytes=64)
             for j in range(BATCH):
                 x_f32 = x_batches[r][:, j, :].bitcast(F32)
                 xt = psum_transposes.tile([P, X_PASSES, 2, P], F32, tag="transposed")
@@ -134,99 +124,79 @@ def tile_kan_kernel(tc, x, W_words, W_scales, b, agg_words, agg_scales, out):
                         )
                 copy_out_of_psum(
                     j,
-                    out=x_grouped[:, j]
-                    .rearrange("p g t s -> p (g t s)")
-                    .bitcast(F32)
-                    .rearrange("p (g t u) -> p g t u", g=X_PASSES, u=2),
+                    out=x_grouped[:, :, j].bitcast(F32),
                     in_=xt[:].rearrange("p g u t -> p g t u"),
                 )
             x_grouped_of[r] = x_grouped
 
         def quantise_x(r):
-            x_codes = work.tile([P, BATCH, X_PASSES, P], U32, align_bytes=64)
-            x_scales = work.tile([P, BATCH, X_PASSES, P], U8, align_bytes=64)
+            x_codes = work.tile([P, X_PASSES, BATCH_TOKENS], U32, align_bytes=64)
+            x_scales = work.tile([P, X_PASSES, BATCH_TOKENS], U8, align_bytes=64)
             nc.vector.quantize_mx(
-                out=x_codes[:].rearrange("p j g t -> p (j g t)").bitcast(FP8X4),
-                scales=x_scales[:].rearrange("p j g t -> p (j g t)"),
-                in_=x_grouped_of[r][:].rearrange("p j g t s -> p (j g t s)"),
+                out=x_codes[:].rearrange("p g t -> p (g t)").bitcast(FP8X4),
+                scales=x_scales[:].rearrange("p g t -> p (g t)"),
+                in_=x_grouped_of[r][:].rearrange("p g j t s -> p (g j t s)"),
             )
             x_mx_of[r] = (x_codes, x_scales)
 
         def first_product(r):
             x_codes, x_scales = x_mx_of[r]
             h_of[r] = []
-            for j in range(BATCH):
-                h = psum_products.tile([P, BRANCHES], F32, tag="product")
+            for f in range(FUNCTIONS):
+                if f % 2 == 0:
+                    h_bank = psum_products.tile([P, 2, BATCH_TOKENS], F32, tag="product")
                 for g in range(X_PASSES):
                     nc.tensor.matmul_mx(
-                        out=h[:],
-                        lhsT=x_codes[:, j, g, :].bitcast(FP8X4),
-                        lhsT_scale=x_scales[:, j, g, :],
-                        rhs=w_words[:, g, :].bitcast(FP8X4),
-                        rhs_scale=planes[:, g, :],
+                        out=h_bank[:, f % 2, :],
+                        lhsT=w_words[:, g, PACK * P * f : PACK * P * (f + 1)].bitcast(FP8X4),
+                        lhsT_scale=planes[:, g, P * f : P * (f + 1)],
+                        rhs=x_codes[:, g, :].bitcast(FP8X4),
+                        rhs_scale=x_scales[:, g, :],
                         start=(g == 0),
                         stop=(g == X_PASSES - 1),
                     )
-                h_of[r].append(h)
-
-        def add_bias(r):
-            biased = work.tile([P, BATCH, PACK, P], F32)
-            for j in range(BATCH):
-                nc.vector.tensor_tensor(
-                    out=biased[:, j],
-                    in0=h_of[r][j][:].rearrange("p (w s) -> p s w", s=PACK),
-                    in1=bias_sorted[:],
-                    op=ALU.add,
-                )
-            biased_of[r] = biased
-
-        def relu(r):
-            activated = work.tile([P, BATCH, PACK, P], F32)
-            nc.vector.tensor_scalar_max(
-                out=activated[:, :, :, 0:QUADRANT],
-                in0=biased_of[r][:, :, :, 0:QUADRANT],
-                scalar1=0.0,
-            )
-            act_of[r] = activated
+                h_of[r].append(h_bank[:, f % 2, :])
 
         def activate(r):
-            functions = ((ACT.Tanh, 1.0), (ACT.Tanh, 0.5), (ACT.Gelu, 1.0))
-            for block, (func, scale) in enumerate(functions, start=1):
-                cols = slice(QUADRANT * block, QUADRANT * (block + 1))
-                nc.scalar.activation(
-                    out=act_of[r][:, :, :, cols],
-                    in_=biased_of[r][:, :, :, cols],
-                    func=func,
-                    scale=scale,
+            h = h_of[r]
+            c_rows = moved.tile([P, FUNCTIONS, BATCH_TOKENS], BF16)
+            half_tanh = work.tile([P, BATCH_TOKENS], F32)
+            nc.scalar.activation(
+                out=c_rows[:, 0, :], in_=h[0], func=ACT.Relu, bias=bias_columns[:, 0:1]
+            )
+            nc.scalar.activation(
+                out=c_rows[:, 1, :], in_=h[1], func=ACT.Tanh, bias=bias_columns[:, 1:2]
+            )
+            nc.scalar.activation(
+                out=half_tanh[:], in_=h[2], func=ACT.Tanh, bias=half_sigmoid_bias[:, 0:1], scale=0.5
+            )
+            nc.scalar.activation(
+                out=c_rows[:, 3, :], in_=h[3], func=ACT.Gelu, bias=bias_columns[:, 3:4]
+            )
+            nc.scalar.activation(
+                out=c_rows[:, 2, :], in_=half_tanh[:], func=ACT.Identity, bias=half_column[:, 0:1], scale=0.5
+            )
+            planar = moved.tile([P, PACK, BATCH_TOKENS], BF16)
+            for f in (0, 1, 3, 2):
+                nc.sync.dma_start(
+                    out=planar[WORD_ROWS * f : WORD_ROWS * (f + 1), :, :], in_=c_rows[:, f, :]
                 )
-
-        def transpose_c(r):
-            ct_of[r] = []
-            for j in range(BATCH):
-                ct = psum_transposes.tile([P, PACK, P], F32, tag="transposed")
-                for s in range(PACK):
-                    nc.tensor.transpose(ct[:, s, :], act_of[r][:, j, s, :], identity[:])
-                ct_of[r].append(ct)
+            planar_of[r] = planar
 
         def group_c(r):
-            c_grouped = work.tile([P, BATCH, P, PACK], BF16, align_bytes=64)
-            for j in range(BATCH):
-                nc.scalar.activation(
-                    out=c_grouped[:, j],
-                    in_=ct_of[r][j][:].rearrange("p s t -> p t s"),
-                    func=ACT.Identity,
-                    scale=c_scale[:, 0:1],
-                    bias=c_bias[:, 0:1],
-                )
+            c_grouped = work.tile([P, BATCH_TOKENS, PACK], BF16, align_bytes=64)
+            nc.vector.tensor_copy(
+                out=c_grouped[:], in_=planar_of[r][:].rearrange("p s t -> p t s")
+            )
             c_grouped_of[r] = c_grouped
 
         def quantise_c(r):
-            c_codes = work.tile([P, BATCH, P], U32, align_bytes=64)
-            c_scales = work.tile([P, BATCH, P], U8, align_bytes=64)
+            c_codes = work.tile([P, BATCH_TOKENS], U32, align_bytes=64)
+            c_scales = work.tile([P, BATCH_TOKENS], U8, align_bytes=64)
             nc.vector.quantize_mx(
-                out=c_codes[:].rearrange("p j t -> p (j t)").bitcast(FP8X4),
-                scales=c_scales[:].rearrange("p j t -> p (j t)"),
-                in_=c_grouped_of[r][:].rearrange("p j t s -> p (j t s)"),
+                out=c_codes[:].bitcast(FP8X4),
+                scales=c_scales[:],
+                in_=c_grouped_of[r][:].rearrange("p t s -> p (t s)"),
             )
             c_mx_of[r] = (c_codes, c_scales)
 
@@ -237,8 +207,8 @@ def tile_kan_kernel(tc, x, W_words, W_scales, b, agg_words, agg_scales, out):
                 o = psum_products.tile([P, D_OUT], F32, tag="product")
                 nc.tensor.matmul_mx(
                     out=o[:],
-                    lhsT=c_codes[:, j, :].bitcast(FP8X4),
-                    lhsT_scale=c_scales[:, j, :],
+                    lhsT=c_codes[:, P * j : P * (j + 1)].bitcast(FP8X4),
+                    lhsT_scale=c_scales[:, P * j : P * (j + 1)],
                     rhs=a_words[:].bitcast(FP8X4),
                     rhs_scale=planes[:, AGG_PLANE, :],
                     start=True,
@@ -247,36 +217,32 @@ def tile_kan_kernel(tc, x, W_words, W_scales, b, agg_words, agg_scales, out):
                 o_of[r].append(o)
 
         def store(r):
+            result = moved.tile([P, BATCH, D_OUT], F32)
             for j in range(BATCH):
-                result = out_pool.tile([P, D_OUT], F32)
-                copy_out_of_psum(j, out=result[:], in_=o_of[r][j][:])
-                nc.sync.dma_start(out=out_tiles[:, BATCH * r + j, :], in_=result[:])
+                copy_out_of_psum(j, out=result[:, j, :], in_=o_of[r][j][:])
+            nc.sync.dma_start(out=out_tiles[:, BATCH * r : BATCH * (r + 1), :], in_=result[:])
 
         def in_range(batch):
             return 0 <= batch < ROUNDS
 
-        for r in range(ROUNDS + 5):
+        for r in range(ROUNDS + 6):
+            if in_range(r - 4):
+                group_c(r - 4)
             if in_range(r - 1):
                 quantise_x(r - 1)
-            if in_range(r - 2):
-                add_bias(r - 2)
             if in_range(r - 4):
                 quantise_c(r - 4)
-            if in_range(r - 5):
-                store(r - 5)
             if in_range(r - 2):
-                relu(r - 2)
+                activate(r - 2)
+            if in_range(r - 6):
+                store(r - 6)
+            if in_range(r + LOADS_AHEAD):
+                load_x(r + LOADS_AHEAD)
             if in_range(r):
                 transpose_x(r)
             if r == 1:
-                spread_bias()
-            if in_range(r - 3):
-                transpose_c(r - 3)
-            if in_range(r - 2):
-                activate(r - 2)
-            if in_range(r - 3):
-                group_c(r - 3)
+                turn_bias()
             if in_range(r - 1):
                 first_product(r - 1)
-            if in_range(r - 4):
-                second_product(r - 4)
+            if in_range(r - 5):
+                second_product(r - 5)

@@ -10,6 +10,7 @@ U32 = mybir.dt.uint32
 U8 = mybir.dt.uint8
 FP8X4 = mybir.dt.float8_e4m3fn_x4
 ACT = mybir.ActivationFunctionType
+ALU = mybir.AluOpType
 
 P = 128
 PACK = 4
@@ -23,7 +24,7 @@ BATCH_TOKENS = BATCH * P
 ROUNDS = TILES // BATCH
 WORD_ROWS = P // PACK
 AGG_PLANE = X_PASSES
-LOADS_AHEAD = 4
+LOADS_AHEAD = 3
 
 FLOPS = 2 * TOKENS * D_IN * BRANCHES + 2 * TOKENS * BRANCHES * D_OUT
 
@@ -48,8 +49,6 @@ def tile_kan_kernel(tc, x, W_words, W_scales, b, agg_words, agg_scales, out):
         nc.vector.memset(bias_rows[:], 0.0)
         zero_column = consts.tile([P, 1], F32)
         nc.vector.memset(zero_column[:], 0.0)
-        half_column = consts.tile([P, 1], F32)
-        nc.vector.memset(half_column[:], 0.5)
         identity = consts.tile([P, P], F32)
         make_identity(nc, identity[:])
 
@@ -58,9 +57,13 @@ def tile_kan_kernel(tc, x, W_words, W_scales, b, agg_words, agg_scales, out):
 
         x_batches = []
 
-        def load_x(r):
+        def load_x(r, tiles_per_load=BATCH):
             x_batch = x_pool.tile([P, BATCH, D_IN], BF16)
-            nc.sync.dma_start(out=x_batch[:], in_=x_tiles[:, BATCH * r : BATCH * (r + 1), :])
+            for j in range(0, BATCH, tiles_per_load):
+                nc.sync.dma_start(
+                    out=x_batch[:, j : j + tiles_per_load, :],
+                    in_=x_tiles[:, BATCH * r + j : BATCH * r + j + tiles_per_load, :],
+                )
             x_batches.append(x_batch)
 
         def load_scales(plane_slots, scale_rows):
@@ -72,16 +75,16 @@ def tile_kan_kernel(tc, x, W_words, W_scales, b, agg_words, agg_scales, out):
                     .bitcast(I32),
                 )
 
-        load_x(0)
-        load_x(1)
+        load_x(0, tiles_per_load=1)
+        bias_stage = consts.tile([FUNCTIONS, P], BF16)
+        nc.sync.dma_start(out=bias_stage[:], in_=b.rearrange("(f m) -> f m", f=FUNCTIONS))
         load_scales(slice(0, X_PASSES), W_scales)
+        load_x(1)
         w_words = consts.tile([P, X_PASSES, PACK * BRANCHES], U8, align_bytes=64)
         nc.sync.dma_start(
             out=w_words[:].bitcast(I32),
             in_=W_words.rearrange("g p n t -> p g (n t)").bitcast(I32),
         )
-        bias_stage = consts.tile([FUNCTIONS, P], BF16)
-        nc.sync.dma_start(out=bias_stage[:], in_=b.rearrange("(f m) -> f m", f=FUNCTIONS))
         for r in range(2, LOADS_AHEAD):
             load_x(r)
         load_scales(slice(AGG_PLANE, AGG_PLANE + 1), agg_scales)
@@ -94,8 +97,10 @@ def tile_kan_kernel(tc, x, W_words, W_scales, b, agg_words, agg_scales, out):
         bias_columns = consts.tile([P, FUNCTIONS], F32)
         half_sigmoid_bias = consts.tile([P, 1], F32)
 
-        def turn_bias():
+        def stage_bias():
             nc.vector.tensor_copy(out=bias_rows[0:FUNCTIONS, :], in_=bias_stage[:])
+
+        def turn_bias():
             bias_bank = psum_transposes.tile([P, P], F32, tag="transposed")
             nc.tensor.transpose(bias_bank[:], bias_rows[:], identity[:])
             nc.vector.tensor_copy(out=bias_columns[:], in_=bias_bank[:, 0:FUNCTIONS])
@@ -103,8 +108,8 @@ def tile_kan_kernel(tc, x, W_words, W_scales, b, agg_words, agg_scales, out):
                 out=half_sigmoid_bias[:], in0=bias_columns[:, 2:3], scalar1=0.5
             )
 
-        def copy_out_of_psum(j, out, in_):
-            if j % 2 == 0:
+        def copy_out_of_psum(on_scalar, out, in_):
+            if on_scalar:
                 nc.scalar.copy(out=out, in_=in_)
             else:
                 nc.vector.tensor_copy(out=out, in_=in_)
@@ -123,7 +128,7 @@ def tile_kan_kernel(tc, x, W_words, W_scales, b, agg_words, agg_scales, out):
                             xt[:, g, u, :], x_f32[:, first + u : first + K_PASS // 2 : 2], identity[:]
                         )
                 copy_out_of_psum(
-                    j,
+                    j == 0 or r == ROUNDS - 1,
                     out=x_grouped[:, :, j].bitcast(F32),
                     in_=xt[:].rearrange("p g u t -> p g t u"),
                 )
@@ -173,8 +178,8 @@ def tile_kan_kernel(tc, x, W_words, W_scales, b, agg_words, agg_scales, out):
             nc.scalar.activation(
                 out=c_rows[:, 3, :], in_=h[3], func=ACT.Gelu, bias=bias_columns[:, 3:4]
             )
-            nc.scalar.activation(
-                out=c_rows[:, 2, :], in_=half_tanh[:], func=ACT.Identity, bias=half_column[:, 0:1], scale=0.5
+            nc.gpsimd.tensor_scalar(
+                out=c_rows[:, 2, :], in0=half_tanh[:], scalar1=0.5, scalar2=0.5, op0=ALU.mult, op1=ALU.add
             )
             planar = moved.tile([P, PACK, BATCH_TOKENS], BF16)
             for f in (0, 1, 3, 2):
@@ -219,28 +224,30 @@ def tile_kan_kernel(tc, x, W_words, W_scales, b, agg_words, agg_scales, out):
         def store(r):
             result = moved.tile([P, BATCH, D_OUT], F32)
             for j in range(BATCH):
-                copy_out_of_psum(j, out=result[:, j, :], in_=o_of[r][j][:])
+                copy_out_of_psum(j == 0 or (r >= ROUNDS // 2 and r % 2 == 0), out=result[:, j, :], in_=o_of[r][j][:])
             nc.sync.dma_start(out=out_tiles[:, BATCH * r : BATCH * (r + 1), :], in_=result[:])
 
         def in_range(batch):
             return 0 <= batch < ROUNDS
 
         for r in range(ROUNDS + 6):
-            if in_range(r - 4):
-                group_c(r - 4)
+            if r == 0:
+                stage_bias()
             if in_range(r - 1):
                 quantise_x(r - 1)
-            if in_range(r - 4):
-                quantise_c(r - 4)
+            if LOADS_AHEAD <= r + 2 < ROUNDS:
+                load_x(r + 2)
             if in_range(r - 2):
                 activate(r - 2)
             if in_range(r - 6):
                 store(r - 6)
-            if in_range(r + LOADS_AHEAD):
-                load_x(r + LOADS_AHEAD)
+            if in_range(r - 4):
+                group_c(r - 4)
+            if in_range(r - 4):
+                quantise_c(r - 4)
             if in_range(r):
                 transpose_x(r)
-            if r == 1:
+            if r == 0:
                 turn_bias()
             if in_range(r - 1):
                 first_product(r - 1)

@@ -191,7 +191,8 @@ def tile_kan_kernel(tc, x, W_words, W_scales, b, agg_words, agg_scales, out):
         def group_c(r):
             c_grouped = work.tile([P, BATCH_TOKENS, PACK], BF16, align_bytes=64)
             nc.vector.tensor_copy(
-                out=c_grouped[:], in_=planar_of[r][:].rearrange("p s t -> p t s")
+                out=c_grouped[:].rearrange("p (n i) s -> p n s i", i=4),
+                in_=planar_of[r][:].rearrange("p s (n i) -> p n s i", i=4),
             )
             c_grouped_of[r] = c_grouped
 

@@ -224,9 +224,15 @@ def tile_kan_kernel(tc, x, W_words, W_scales, b, agg_words, agg_scales, out):
 
         def store(r):
             result = moved.tile([P, BATCH, D_OUT], F32)
+            tiles_per_store = BATCH if r < ROUNDS - 1 else 1
             for j in range(BATCH):
                 copy_out_of_psum(j == 0 or (r >= ROUNDS // 2 and r % 2 == 0), out=result[:, j, :], in_=o_of[r][j][:])
-            nc.sync.dma_start(out=out_tiles[:, BATCH * r : BATCH * (r + 1), :], in_=result[:])
+                if (j + 1) % tiles_per_store == 0:
+                    first = j + 1 - tiles_per_store
+                    nc.sync.dma_start(
+                        out=out_tiles[:, BATCH * r + first : BATCH * r + j + 1, :],
+                        in_=result[:, first : j + 1, :],
+                    )
 
         def in_range(batch):
             return 0 <= batch < ROUNDS
@@ -244,10 +250,10 @@ def tile_kan_kernel(tc, x, W_words, W_scales, b, agg_words, agg_scales, out):
                 store(r - 6)
             if in_range(r - 4):
                 group_c(r - 4)
-            if in_range(r - 4):
-                quantise_c(r - 4)
             if in_range(r):
                 transpose_x(r)
+            if in_range(r - 4):
+                quantise_c(r - 4)
             if r == 0:
                 turn_bias()
             if in_range(r - 1):

@@ -24,6 +24,7 @@ BATCH_TOKENS = BATCH * P
 ROUNDS = TILES // BATCH
 WORD_ROWS = P // PACK
 AGG_PLANE = X_PASSES
+REGROUP_LAG = 4
 LOADS_AHEAD = 3
 
 FLOPS = 2 * TOKENS * D_IN * BRANCHES + 2 * TOKENS * BRANCHES * D_OUT
@@ -128,7 +129,7 @@ def tile_kan_kernel(tc, x, W_words, W_scales, b, agg_words, agg_scales, out):
                             xt[:, g, u, :], x_f32[:, first + u : first + K_PASS // 2 : 2], identity[:]
                         )
                 copy_out_of_psum(
-                    j == 0 or r == ROUNDS - 1,
+                    j == 1 if r == 0 else (j == 0 or r == ROUNDS - 1),
                     out=x_grouped[:, :, j].bitcast(F32),
                     in_=xt[:].rearrange("p g u t -> p g t u"),
                 )
@@ -188,51 +189,57 @@ def tile_kan_kernel(tc, x, W_words, W_scales, b, agg_words, agg_scales, out):
                 )
             planar_of[r] = planar
 
+        def token_pieces(r):
+            size = BATCH_TOKENS if in_range(r + REGROUP_LAG + 1) else P
+            return [slice(first, first + size) for first in range(0, BATCH_TOKENS, size)]
+
         def group_c(r):
             c_grouped = work.tile([P, BATCH_TOKENS, PACK], BF16, align_bytes=64)
-            nc.vector.tensor_copy(
-                out=c_grouped[:].rearrange("p (n i) s -> p n s i", i=4),
-                in_=planar_of[r][:].rearrange("p s (n i) -> p n s i", i=4),
-            )
+            for piece in token_pieces(r):
+                nc.vector.tensor_copy(
+                    out=c_grouped[:, piece, :].rearrange("p (n i) s -> p n s i", i=4),
+                    in_=planar_of[r][:, :, piece].rearrange("p s (n i) -> p n s i", i=4),
+                )
             c_grouped_of[r] = c_grouped
 
         def quantise_c(r):
             c_codes = work.tile([P, BATCH_TOKENS], U32, align_bytes=64)
             c_scales = work.tile([P, BATCH_TOKENS], U8, align_bytes=64)
-            nc.vector.quantize_mx(
-                out=c_codes[:].bitcast(FP8X4),
-                scales=c_scales[:],
-                in_=c_grouped_of[r][:].rearrange("p t s -> p (t s)"),
-            )
+            for piece in token_pieces(r):
+                nc.vector.quantize_mx(
+                    out=c_codes[:, piece].bitcast(FP8X4),
+                    scales=c_scales[:, piece],
+                    in_=c_grouped_of[r][:, piece, :].rearrange("p t s -> p (t s)"),
+                )
             c_mx_of[r] = (c_codes, c_scales)
 
         def second_product(r):
             c_codes, c_scales = c_mx_of[r]
+            width = D_OUT if r < ROUNDS - 1 else D_OUT // 2
             o_of[r] = []
             for j in range(BATCH):
-                o = psum_products.tile([P, D_OUT], F32, tag="product")
-                nc.tensor.matmul_mx(
-                    out=o[:],
-                    lhsT=c_codes[:, P * j : P * (j + 1)].bitcast(FP8X4),
-                    lhsT_scale=c_scales[:, P * j : P * (j + 1)],
-                    rhs=a_words[:].bitcast(FP8X4),
-                    rhs_scale=planes[:, AGG_PLANE, :],
-                    start=True,
-                    stop=True,
-                )
-                o_of[r].append(o)
+                for first in range(0, D_OUT, width):
+                    o = psum_products.tile([P, width], F32, tag="product")
+                    nc.tensor.matmul_mx(
+                        out=o[:],
+                        lhsT=c_codes[:, P * j : P * (j + 1)].bitcast(FP8X4),
+                        lhsT_scale=c_scales[:, P * j : P * (j + 1)],
+                        rhs=a_words[:, PACK * first : PACK * (first + width)].bitcast(FP8X4),
+                        rhs_scale=planes[:, AGG_PLANE, first : first + width],
+                        start=True,
+                        stop=True,
+                    )
+                    o_of[r].append((j, slice(first, first + width), o))
 
         def store(r):
             result = moved.tile([P, BATCH, D_OUT], F32)
-            tiles_per_store = BATCH if r < ROUNDS - 1 else 1
-            for j in range(BATCH):
-                copy_out_of_psum(j == 0 or (r >= ROUNDS // 2 and r % 2 == 0), out=result[:, j, :], in_=o_of[r][j][:])
-                if (j + 1) % tiles_per_store == 0:
-                    first = j + 1 - tiles_per_store
-                    nc.sync.dma_start(
-                        out=out_tiles[:, BATCH * r + first : BATCH * r + j + 1, :],
-                        in_=result[:, first : j + 1, :],
-                    )
+            scalar_copies_all = r >= ROUNDS // 2 and r % 2 == 0
+            for index, (j, columns, o) in enumerate(o_of[r]):
+                copy_out_of_psum(index % 2 == 0 or scalar_copies_all, out=result[:, j, columns], in_=o[:])
+                if r == ROUNDS - 1 and columns.stop == D_OUT:
+                    nc.sync.dma_start(out=out_tiles[:, BATCH * r + j, :], in_=result[:, j, :])
+            if r < ROUNDS - 1:
+                nc.sync.dma_start(out=out_tiles[:, BATCH * r : BATCH * (r + 1), :], in_=result[:])
 
         def in_range(batch):
             return 0 <= batch < ROUNDS
@@ -248,12 +255,12 @@ def tile_kan_kernel(tc, x, W_words, W_scales, b, agg_words, agg_scales, out):
                 activate(r - 2)
             if in_range(r - 6):
                 store(r - 6)
-            if in_range(r - 4):
-                group_c(r - 4)
+            if in_range(r - REGROUP_LAG):
+                group_c(r - REGROUP_LAG)
             if in_range(r):
                 transpose_x(r)
-            if in_range(r - 4):
-                quantise_c(r - 4)
+            if in_range(r - REGROUP_LAG):
+                quantise_c(r - REGROUP_LAG)
             if r == 0:
                 turn_bias()
             if in_range(r - 1):

@@ -25,6 +25,8 @@ ROUNDS = TILES // BATCH
 WORD_ROWS = P // PACK
 AGG_PLANE = X_PASSES
 REGROUP_LAG = 4
+FUNCTION_ORDER = (2, 0, 1, 3)
+MOVE_ORDER = (0, 2, 1, 3)
 LOADS_AHEAD = 3
 
 FLOPS = 2 * TOKENS * D_IN * BRANCHES + 2 * TOKENS * BRANCHES * D_OUT
@@ -38,8 +40,8 @@ def tile_kan_kernel(tc, x, W_words, W_scales, b, agg_words, agg_scales, out):
     with ExitStack() as stack:
         consts = stack.enter_context(tc.tile_pool(name="consts", bufs=1))
         x_pool = stack.enter_context(tc.tile_pool(name="x", bufs=ROUNDS))
-        work = stack.enter_context(tc.tile_pool(name="work", bufs=2))
-        moved = stack.enter_context(tc.tile_pool(name="moved", bufs=4))
+        work = stack.enter_context(tc.tile_pool(name="work", bufs=ROUNDS))
+        moved = stack.enter_context(tc.tile_pool(name="moved", bufs=ROUNDS))
         psum_transposes = stack.enter_context(tc.psum_pool(name="psum_transposes", bufs=4))
         psum_products = stack.enter_context(tc.psum_pool(name="psum_products", bufs=4))
         stack.enter_context(tc.manual_schedule())
@@ -147,13 +149,13 @@ def tile_kan_kernel(tc, x, W_words, W_scales, b, agg_words, agg_scales, out):
 
         def first_product(r):
             x_codes, x_scales = x_mx_of[r]
-            h_of[r] = []
-            for f in range(FUNCTIONS):
-                if f % 2 == 0:
+            h_of[r] = {}
+            for place, f in enumerate(FUNCTION_ORDER):
+                if place % 2 == 0:
                     h_bank = psum_products.tile([P, 2, BATCH_TOKENS], F32, tag="product")
                 for g in range(X_PASSES):
                     nc.tensor.matmul_mx(
-                        out=h_bank[:, f % 2, :],
+                        out=h_bank[:, place % 2, :],
                         lhsT=w_words[:, g, PACK * P * f : PACK * P * (f + 1)].bitcast(FP8X4),
                         lhsT_scale=planes[:, g, P * f : P * (f + 1)],
                         rhs=x_codes[:, g, :].bitcast(FP8X4),
@@ -161,29 +163,29 @@ def tile_kan_kernel(tc, x, W_words, W_scales, b, agg_words, agg_scales, out):
                         start=(g == 0),
                         stop=(g == X_PASSES - 1),
                     )
-                h_of[r].append(h_bank[:, f % 2, :])
+                h_of[r][f] = h_bank[:, place % 2, :]
 
         def activate(r):
             h = h_of[r]
             c_rows = moved.tile([P, FUNCTIONS, BATCH_TOKENS], BF16)
             half_tanh = work.tile([P, BATCH_TOKENS], F32)
-            nc.scalar.activation(
-                out=c_rows[:, 0, :], in_=h[0], func=ACT.Relu, bias=bias_columns[:, 0:1]
-            )
-            nc.scalar.activation(
-                out=c_rows[:, 1, :], in_=h[1], func=ACT.Tanh, bias=bias_columns[:, 1:2]
-            )
-            nc.scalar.activation(
-                out=half_tanh[:], in_=h[2], func=ACT.Tanh, bias=half_sigmoid_bias[:, 0:1], scale=0.5
-            )
-            nc.scalar.activation(
-                out=c_rows[:, 3, :], in_=h[3], func=ACT.Gelu, bias=bias_columns[:, 3:4]
-            )
-            nc.gpsimd.tensor_scalar(
-                out=c_rows[:, 2, :], in0=half_tanh[:], scalar1=0.5, scalar2=0.5, op0=ALU.mult, op1=ALU.add
-            )
+            for f in FUNCTION_ORDER:
+                if f == 2:
+                    nc.scalar.activation(
+                        out=half_tanh[:], in_=h[2], func=ACT.Tanh, bias=half_sigmoid_bias[:, 0:1], scale=0.5
+                    )
+                    nc.gpsimd.tensor_scalar(
+                        out=c_rows[:, 2, :], in0=half_tanh[:], scalar1=0.5, scalar2=0.5, op0=ALU.mult, op1=ALU.add
+                    )
+                else:
+                    nc.scalar.activation(
+                        out=c_rows[:, f, :],
+                        in_=h[f],
+                        func={0: ACT.Relu, 1: ACT.Tanh, 3: ACT.Gelu}[f],
+                        bias=bias_columns[:, f : f + 1],
+                    )
             planar = moved.tile([P, PACK, BATCH_TOKENS], BF16)
-            for f in (0, 1, 3, 2):
+            for f in MOVE_ORDER:
                 nc.sync.dma_start(
                     out=planar[WORD_ROWS * f : WORD_ROWS * (f + 1), :, :], in_=c_rows[:, f, :]
                 )

@@ -25,9 +25,9 @@ ROUNDS = TILES // BATCH
 WORD_ROWS = P // PACK
 AGG_PLANE = X_PASSES
 REGROUP_LAG = 4
-FUNCTION_ORDER = (2, 0, 1, 3)
-MOVE_ORDER = (0, 2, 1, 3)
-LOADS_AHEAD = 3
+FUNCTION_ORDER = (2, 1, 0, 3)
+MOVE_ORDER = (1, 2, 0, 3)
+LOADS_AHEAD = 6
 
 FLOPS = 2 * TOKENS * D_IN * BRANCHES + 2 * TOKENS * BRANCHES * D_OUT
 
@@ -88,14 +88,15 @@ def tile_kan_kernel(tc, x, W_words, W_scales, b, agg_words, agg_scales, out):
             out=w_words[:].bitcast(I32),
             in_=W_words.rearrange("g p n t -> p g (n t)").bitcast(I32),
         )
-        for r in range(2, LOADS_AHEAD):
-            load_x(r)
+        load_x(2)
         load_scales(slice(AGG_PLANE, AGG_PLANE + 1), agg_scales)
         a_words = consts.tile([P, PACK * D_OUT], U8, align_bytes=64)
         nc.sync.dma_start(
             out=a_words[:].bitcast(I32),
             in_=agg_words[0].rearrange("p n t -> p (n t)").bitcast(I32),
         )
+        for r in range(3, LOADS_AHEAD):
+            load_x(r)
 
         bias_columns = consts.tile([P, FUNCTIONS], F32)
         half_sigmoid_bias = consts.tile([P, 1], F32)
@@ -117,25 +118,29 @@ def tile_kan_kernel(tc, x, W_words, W_scales, b, agg_words, agg_scales, out):
             else:
                 nc.vector.tensor_copy(out=out, in_=in_)
 
-        x_grouped_of, x_mx_of, h_of, planar_of, c_grouped_of, c_mx_of, o_of = {}, {}, {}, {}, {}, {}, {}
+        xt_of, x_grouped_of, x_mx_of, h_of, c_rows_of, planar_of, c_grouped_of, c_mx_of, o_of, result_of = (
+            {}, {}, {}, {}, {}, {}, {}, {}, {}, {}
+        )
 
-        def transpose_x(r):
-            x_grouped = work.tile([P, X_PASSES, BATCH, P, PACK], BF16, align_bytes=64)
-            for j in range(BATCH):
-                x_f32 = x_batches[r][:, j, :].bitcast(F32)
-                xt = psum_transposes.tile([P, X_PASSES, 2, P], F32, tag="transposed")
-                for g in range(X_PASSES):
-                    first = g * K_PASS // 2
-                    for u in range(2):
-                        nc.tensor.transpose(
-                            xt[:, g, u, :], x_f32[:, first + u : first + K_PASS // 2 : 2], identity[:]
-                        )
-                copy_out_of_psum(
-                    j == 1 if r == 0 else (j == 0 or r == ROUNDS - 1),
-                    out=x_grouped[:, :, j].bitcast(F32),
-                    in_=xt[:].rearrange("p g u t -> p g t u"),
-                )
-            x_grouped_of[r] = x_grouped
+        def transpose_x(r, j):
+            x_f32 = x_batches[r][:, j, :].bitcast(F32)
+            xt = psum_transposes.tile([P, X_PASSES, 2, P], F32, tag="transposed")
+            for g in range(X_PASSES):
+                first = g * K_PASS // 2
+                for u in range(2):
+                    nc.tensor.transpose(
+                        xt[:, g, u, :], x_f32[:, first + u : first + K_PASS // 2 : 2], identity[:]
+                    )
+            xt_of[r, j] = xt
+
+        def group_x(r, j):
+            if r not in x_grouped_of:
+                x_grouped_of[r] = work.tile([P, X_PASSES, BATCH, P, PACK], BF16, align_bytes=64, name="x_grouped")
+            copy_out_of_psum(
+                j == (1 if r < 2 else 0),
+                out=x_grouped_of[r][:, :, j].bitcast(F32),
+                in_=xt_of[r, j][:].rearrange("p g u t -> p g t u"),
+            )
 
         def quantise_x(r):
             x_codes = work.tile([P, X_PASSES, BATCH_TOKENS], U32, align_bytes=64)
@@ -147,15 +152,13 @@ def tile_kan_kernel(tc, x, W_words, W_scales, b, agg_words, agg_scales, out):
             )
             x_mx_of[r] = (x_codes, x_scales)
 
-        def first_product(r):
+        def first_product(r, half):
             x_codes, x_scales = x_mx_of[r]
-            h_of[r] = {}
-            for place, f in enumerate(FUNCTION_ORDER):
-                if place % 2 == 0:
-                    h_bank = psum_products.tile([P, 2, BATCH_TOKENS], F32, tag="product")
+            h_bank = psum_products.tile([P, 2, BATCH_TOKENS], F32, tag="product")
+            for place, f in enumerate(FUNCTION_ORDER[2 * half : 2 * half + 2]):
                 for g in range(X_PASSES):
                     nc.tensor.matmul_mx(
-                        out=h_bank[:, place % 2, :],
+                        out=h_bank[:, place, :],
                         lhsT=w_words[:, g, PACK * P * f : PACK * P * (f + 1)].bitcast(FP8X4),
                         lhsT_scale=planes[:, g, P * f : P * (f + 1)],
                         rhs=x_codes[:, g, :].bitcast(FP8X4),
@@ -163,10 +166,10 @@ def tile_kan_kernel(tc, x, W_words, W_scales, b, agg_words, agg_scales, out):
                         start=(g == 0),
                         stop=(g == X_PASSES - 1),
                     )
-                h_of[r][f] = h_bank[:, place % 2, :]
+                h_of[r, f] = h_bank[:, place, :]
 
         def activate(r):
-            h = h_of[r]
+            h = {f: h_of[r, f] for f in FUNCTION_ORDER}
             c_rows = moved.tile([P, FUNCTIONS, BATCH_TOKENS], BF16)
             half_tanh = work.tile([P, BATCH_TOKENS], F32)
             for f in FUNCTION_ORDER:
@@ -184,6 +187,10 @@ def tile_kan_kernel(tc, x, W_words, W_scales, b, agg_words, agg_scales, out):
                         func={0: ACT.Relu, 1: ACT.Tanh, 3: ACT.Gelu}[f],
                         bias=bias_columns[:, f : f + 1],
                     )
+            c_rows_of[r] = c_rows
+
+        def move_c(r):
+            c_rows = c_rows_of[r]
             planar = moved.tile([P, PACK, BATCH_TOKENS], BF16)
             for f in MOVE_ORDER:
                 nc.sync.dma_start(
@@ -192,7 +199,7 @@ def tile_kan_kernel(tc, x, W_words, W_scales, b, agg_words, agg_scales, out):
             planar_of[r] = planar
 
         def token_pieces(r):
-            size = BATCH_TOKENS if in_range(r + REGROUP_LAG + 1) else P
+            size = BATCH_TOKENS if r < ROUNDS // 2 else P
             return [slice(first, first + size) for first in range(0, BATCH_TOKENS, size)]
 
         def group_c(r):
@@ -215,57 +222,58 @@ def tile_kan_kernel(tc, x, W_words, W_scales, b, agg_words, agg_scales, out):
                 )
             c_mx_of[r] = (c_codes, c_scales)
 
-        def second_product(r):
+        def second_product(r, j):
             c_codes, c_scales = c_mx_of[r]
             width = D_OUT if r < ROUNDS - 1 else D_OUT // 2
-            o_of[r] = []
-            for j in range(BATCH):
-                for first in range(0, D_OUT, width):
-                    o = psum_products.tile([P, width], F32, tag="product")
-                    nc.tensor.matmul_mx(
-                        out=o[:],
-                        lhsT=c_codes[:, P * j : P * (j + 1)].bitcast(FP8X4),
-                        lhsT_scale=c_scales[:, P * j : P * (j + 1)],
-                        rhs=a_words[:, PACK * first : PACK * (first + width)].bitcast(FP8X4),
-                        rhs_scale=planes[:, AGG_PLANE, first : first + width],
-                        start=True,
-                        stop=True,
-                    )
-                    o_of[r].append((j, slice(first, first + width), o))
+            o_of[r, j] = []
+            for first in range(0, D_OUT, width):
+                o = psum_products.tile([P, width], F32, tag="product")
+                nc.tensor.matmul_mx(
+                    out=o[:],
+                    lhsT=c_codes[:, P * j : P * (j + 1)].bitcast(FP8X4),
+                    lhsT_scale=c_scales[:, P * j : P * (j + 1)],
+                    rhs=a_words[:, PACK * first : PACK * (first + width)].bitcast(FP8X4),
+                    rhs_scale=planes[:, AGG_PLANE, first : first + width],
+                    start=True,
+                    stop=True,
+                )
+                o_of[r, j].append((slice(first, first + width), o))
 
-        def store(r):
-            result = moved.tile([P, BATCH, D_OUT], F32)
-            scalar_copies_all = r >= ROUNDS // 2 and r % 2 == 0
-            for index, (j, columns, o) in enumerate(o_of[r]):
-                copy_out_of_psum(index % 2 == 0 or scalar_copies_all, out=result[:, j, columns], in_=o[:])
-                if r == ROUNDS - 1 and columns.stop == D_OUT:
-                    nc.sync.dma_start(out=out_tiles[:, BATCH * r + j, :], in_=result[:, j, :])
-            if r < ROUNDS - 1:
-                nc.sync.dma_start(out=out_tiles[:, BATCH * r : BATCH * (r + 1), :], in_=result[:])
+        def store(r, j):
+            if j == 0:
+                result_of[r] = moved.tile([P, BATCH, D_OUT], F32, name="result")
+            result = result_of[r]
+            for columns, o in o_of[r, j]:
+                on_scalar = columns.start == 0 if r == ROUNDS - 1 else (r >= ROUNDS // 2 or j == 1)
+                copy_out_of_psum(on_scalar, out=result[:, j, columns], in_=o[:])
+            nc.sync.dma_start(out=out_tiles[:, BATCH * r + j, :], in_=result[:, j, :])
 
         def in_range(batch):
             return 0 <= batch < ROUNDS
 
-        for r in range(ROUNDS + 6):
+        def step(function, batch, *args):
+            if in_range(batch):
+                function(batch, *args)
+
+        for r in range(-1, ROUNDS + 6):
             if r == 0:
                 stage_bias()
-            if in_range(r - 1):
-                quantise_x(r - 1)
+            step(activate, r - 2)
+            step(transpose_x, r, 1)
+            step(quantise_x, r - 1)
+            step(move_c, r - 2)
+            if r == 1:
+                turn_bias()
+            step(store, r - 6, 0)
+            step(store, r - 6, 1)
+            step(first_product, r - 1, 0)
+            step(group_c, r - REGROUP_LAG)
+            step(group_x, r, 1)
+            step(group_x, r, 0)
+            step(second_product, r - 5, 0)
+            step(first_product, r - 1, 1)
+            step(quantise_c, r - REGROUP_LAG)
+            step(second_product, r - 5, 1)
+            step(transpose_x, r + 1, 0)
             if LOADS_AHEAD <= r + 2 < ROUNDS:
                 load_x(r + 2)
-            if in_range(r - 2):
-                activate(r - 2)
-            if in_range(r - 6):
-                store(r - 6)
-            if in_range(r - REGROUP_LAG):
-                group_c(r - REGROUP_LAG)
-            if in_range(r):
-                transpose_x(r)
-            if in_range(r - REGROUP_LAG):
-                quantise_c(r - REGROUP_LAG)
-            if r == 0:
-                turn_bias()
-            if in_range(r - 1):
-                first_product(r - 1)
-            if in_range(r - 5):
-                second_product(r - 5)

@@ -25,9 +25,10 @@ ROUNDS = TILES // BATCH
 WORD_ROWS = P // PACK
 AGG_PLANE = X_PASSES
 REGROUP_LAG = 4
-FUNCTION_ORDER = (2, 1, 0, 3)
-MOVE_ORDER = (1, 2, 0, 3)
-LOADS_AHEAD = 6
+FUNCTION_ORDER = (0, 1, 2, 3)
+MOVE_ORDER = (0, 3, 1, 2)
+SINGLE_STORES = 4
+LOADS_AHEAD = 3
 
 FLOPS = 2 * TOKENS * D_IN * BRANCHES + 2 * TOKENS * BRANCHES * D_OUT
 
@@ -42,8 +43,8 @@ def tile_kan_kernel(tc, x, W_words, W_scales, b, agg_words, agg_scales, out):
         x_pool = stack.enter_context(tc.tile_pool(name="x", bufs=ROUNDS))
         work = stack.enter_context(tc.tile_pool(name="work", bufs=ROUNDS))
         moved = stack.enter_context(tc.tile_pool(name="moved", bufs=ROUNDS))
-        psum_transposes = stack.enter_context(tc.psum_pool(name="psum_transposes", bufs=4))
-        psum_products = stack.enter_context(tc.psum_pool(name="psum_products", bufs=4))
+        psum_transposes = stack.enter_context(tc.psum_pool(name="psum_transposes", bufs=3))
+        psum_products = stack.enter_context(tc.psum_pool(name="psum_products", bufs=5))
         stack.enter_context(tc.manual_schedule())
 
         planes = consts.tile([P, X_PASSES + 1, BRANCHES], U8, align_bytes=64)
@@ -137,7 +138,7 @@ def tile_kan_kernel(tc, x, W_words, W_scales, b, agg_words, agg_scales, out):
             if r not in x_grouped_of:
                 x_grouped_of[r] = work.tile([P, X_PASSES, BATCH, P, PACK], BF16, align_bytes=64, name="x_grouped")
             copy_out_of_psum(
-                j == (1 if r < 2 else 0),
+                (True if r < 2 else j == 1) or r >= ROUNDS - 1,
                 out=x_grouped_of[r][:, :, j].bitcast(F32),
                 in_=xt_of[r, j][:].rearrange("p g u t -> p g t u"),
             )
@@ -199,7 +200,7 @@ def tile_kan_kernel(tc, x, W_words, W_scales, b, agg_words, agg_scales, out):
             planar_of[r] = planar
 
         def token_pieces(r):
-            size = BATCH_TOKENS if r < ROUNDS // 2 else P
+            size = BATCH_TOKENS if r < 3 else P
             return [slice(first, first + size) for first in range(0, BATCH_TOKENS, size)]
 
         def group_c(r):
@@ -240,13 +241,18 @@ def tile_kan_kernel(tc, x, W_words, W_scales, b, agg_words, agg_scales, out):
                 o_of[r, j].append((slice(first, first + width), o))
 
         def store(r, j):
-            if j == 0:
+            if r not in result_of:
                 result_of[r] = moved.tile([P, BATCH, D_OUT], F32, name="result")
             result = result_of[r]
             for columns, o in o_of[r, j]:
-                on_scalar = columns.start == 0 if r == ROUNDS - 1 else (r >= ROUNDS // 2 or j == 1)
+                on_scalar = (columns.start == 0) == (j == 0) if r == ROUNDS - 1 else (r >= 4 or j == 1)
                 copy_out_of_psum(on_scalar, out=result[:, j, columns], in_=o[:])
-            nc.sync.dma_start(out=out_tiles[:, BATCH * r + j, :], in_=result[:, j, :])
+            if r >= SINGLE_STORES:
+                nc.sync.dma_start(out=out_tiles[:, BATCH * r + j, :], in_=result[:, j, :])
+
+        def store_batch(r):
+            if r < SINGLE_STORES:
+                nc.sync.dma_start(out=out_tiles[:, BATCH * r : BATCH * (r + 1), :], in_=result_of[r][:])
 
         def in_range(batch):
             return 0 <= batch < ROUNDS
@@ -255,25 +261,26 @@ def tile_kan_kernel(tc, x, W_words, W_scales, b, agg_words, agg_scales, out):
             if in_range(batch):
                 function(batch, *args)
 
-        for r in range(-1, ROUNDS + 6):
+        for r in range(0, ROUNDS + 7):
             if r == 0:
                 stage_bias()
-            step(activate, r - 2)
-            step(transpose_x, r, 1)
             step(quantise_x, r - 1)
-            step(move_c, r - 2)
-            if r == 1:
-                turn_bias()
+            step(transpose_x, r, 0)
             step(store, r - 6, 0)
-            step(store, r - 6, 1)
+            step(transpose_x, r, 1)
+            step(activate, r - 2)
             step(first_product, r - 1, 0)
-            step(group_c, r - REGROUP_LAG)
-            step(group_x, r, 1)
-            step(group_x, r, 0)
-            step(second_product, r - 5, 0)
-            step(first_product, r - 1, 1)
-            step(quantise_c, r - REGROUP_LAG)
-            step(second_product, r - 5, 1)
-            step(transpose_x, r + 1, 0)
             if LOADS_AHEAD <= r + 2 < ROUNDS:
                 load_x(r + 2)
+            step(store, r - 6, 1)
+            if r == 0:
+                turn_bias()
+            step(group_c, r - 4)
+            step(group_x, r, 0)
+            step(group_x, r, 1)
+            step(first_product, r - 1, 1)
+            step(quantise_c, r - 4)
+            step(move_c, r - 2)
+            step(store_batch, r - 6)
+            step(second_product, r - 5, 0)
+            step(second_product, r - 5, 1)

@@ -28,7 +28,7 @@ REGROUP_LAG = 4
 FUNCTION_ORDER = (0, 1, 2, 3)
 MOVE_ORDER = (0, 3, 1, 2)
 SINGLE_STORES = 4
-LOADS_AHEAD = 3
+LOADS_AHEAD = 6
 
 FLOPS = 2 * TOKENS * D_IN * BRANCHES + 2 * TOKENS * BRANCHES * D_OUT
 

from contextlib import ExitStack

import concourse.mybir as mybir
from concourse.masks import make_identity

F32 = mybir.dt.float32
BF16 = mybir.dt.bfloat16
I32 = mybir.dt.int32
U32 = mybir.dt.uint32
U8 = mybir.dt.uint8
FP8X4 = mybir.dt.float8_e4m3fn_x4
ACT = mybir.ActivationFunctionType
ALU = mybir.AluOpType

P = 128
PACK = 4
K_PASS = P * PACK
TOKENS, D_IN, BRANCHES, D_OUT = 2048, 1024, 512, 512
X_PASSES = D_IN // K_PASS
FUNCTIONS = BRANCHES // P
TILES = TOKENS // P
BATCH = 2
BATCH_TOKENS = BATCH * P
ROUNDS = TILES // BATCH
WORD_ROWS = P // PACK
AGG_PLANE = X_PASSES
REGROUP_LAG = 4
FUNCTION_ORDER = (0, 1, 2, 3)
MOVE_ORDER = (0, 3, 1, 2)
SINGLE_STORES = 4
LOADS_AHEAD = 6

FLOPS = 2 * TOKENS * D_IN * BRANCHES + 2 * TOKENS * BRANCHES * D_OUT


def tile_kan_kernel(tc, x, W_words, W_scales, b, agg_words, agg_scales, out):
    nc = tc.nc
    x_tiles = x.rearrange("(p i) k -> p i k", i=TILES)
    out_tiles = out.rearrange("(p i) n -> p i n", i=TILES)

    with ExitStack() as stack:
        consts = stack.enter_context(tc.tile_pool(name="consts", bufs=1))
        x_pool = stack.enter_context(tc.tile_pool(name="x", bufs=ROUNDS))
        work = stack.enter_context(tc.tile_pool(name="work", bufs=ROUNDS))
        moved = stack.enter_context(tc.tile_pool(name="moved", bufs=ROUNDS))
        psum_transposes = stack.enter_context(tc.psum_pool(name="psum_transposes", bufs=3))
        psum_products = stack.enter_context(tc.psum_pool(name="psum_products", bufs=5))
        stack.enter_context(tc.manual_schedule())

        planes = consts.tile([P, X_PASSES + 1, BRANCHES], U8, align_bytes=64)
        nc.vector.memset(planes[:].rearrange("p a n -> p (a n)").bitcast(I32), 0)
        bias_rows = consts.tile([P, P], F32)
        nc.vector.memset(bias_rows[:], 0.0)
        zero_column = consts.tile([P, 1], F32)
        nc.vector.memset(zero_column[:], 0.0)
        identity = consts.tile([P, P], F32)
        make_identity(nc, identity[:])

        table_warmer = consts.tile([P, 1], F32)
        nc.scalar.activation(out=table_warmer[:], in_=zero_column[:], func=ACT.Gelu)

        x_batches = []

        def load_x(r, tiles_per_load=BATCH):
            x_batch = x_pool.tile([P, BATCH, D_IN], BF16)
            for j in range(0, BATCH, tiles_per_load):
                nc.sync.dma_start(
                    out=x_batch[:, j : j + tiles_per_load, :],
                    in_=x_tiles[:, BATCH * r + j : BATCH * r + j + tiles_per_load, :],
                )
            x_batches.append(x_batch)

        def load_scales(plane_slots, scale_rows):
            for quadrant in range(PACK):
                nc.sync.dma_start(
                    out=planes[32 * quadrant : 32 * quadrant + PACK, plane_slots, :].bitcast(I32),
                    in_=scale_rows[:, PACK * quadrant : PACK * (quadrant + 1), :]
                    .rearrange("g q n -> q g n")
                    .bitcast(I32),
                )

        load_x(0, tiles_per_load=1)
        bias_stage = consts.tile([FUNCTIONS, P], BF16)
        nc.sync.dma_start(out=bias_stage[:], in_=b.rearrange("(f m) -> f m", f=FUNCTIONS))
        load_scales(slice(0, X_PASSES), W_scales)
        load_x(1)
        w_words = consts.tile([P, X_PASSES, PACK * BRANCHES], U8, align_bytes=64)
        nc.sync.dma_start(
            out=w_words[:].bitcast(I32),
            in_=W_words.rearrange("g p n t -> p g (n t)").bitcast(I32),
        )
        load_x(2)
        load_scales(slice(AGG_PLANE, AGG_PLANE + 1), agg_scales)
        a_words = consts.tile([P, PACK * D_OUT], U8, align_bytes=64)
        nc.sync.dma_start(
            out=a_words[:].bitcast(I32),
            in_=agg_words[0].rearrange("p n t -> p (n t)").bitcast(I32),
        )
        for r in range(3, LOADS_AHEAD):
            load_x(r)

        bias_columns = consts.tile([P, FUNCTIONS], F32)
        half_sigmoid_bias = consts.tile([P, 1], F32)

        def stage_bias():
            nc.vector.tensor_copy(out=bias_rows[0:FUNCTIONS, :], in_=bias_stage[:])

        def turn_bias():
            bias_bank = psum_transposes.tile([P, P], F32, tag="transposed")
            nc.tensor.transpose(bias_bank[:], bias_rows[:], identity[:])
            nc.vector.tensor_copy(out=bias_columns[:], in_=bias_bank[:, 0:FUNCTIONS])
            nc.vector.tensor_scalar_mul(
                out=half_sigmoid_bias[:], in0=bias_columns[:, 2:3], scalar1=0.5
            )

        def copy_out_of_psum(on_scalar, out, in_):
            if on_scalar:
                nc.scalar.copy(out=out, in_=in_)
            else:
                nc.vector.tensor_copy(out=out, in_=in_)

        xt_of, x_grouped_of, x_mx_of, h_of, c_rows_of, planar_of, c_grouped_of, c_mx_of, o_of, result_of = (
            {}, {}, {}, {}, {}, {}, {}, {}, {}, {}
        )

        def transpose_x(r, j):
            x_f32 = x_batches[r][:, j, :].bitcast(F32)
            xt = psum_transposes.tile([P, X_PASSES, 2, P], F32, tag="transposed")
            for g in range(X_PASSES):
                first = g * K_PASS // 2
                for u in range(2):
                    nc.tensor.transpose(
                        xt[:, g, u, :], x_f32[:, first + u : first + K_PASS // 2 : 2], identity[:]
                    )
            xt_of[r, j] = xt

        def group_x(r, j):
            if r not in x_grouped_of:
                x_grouped_of[r] = work.tile([P, X_PASSES, BATCH, P, PACK], BF16, align_bytes=64, name="x_grouped")
            copy_out_of_psum(
                (True if r < 2 else j == 1) or r >= ROUNDS - 1,
                out=x_grouped_of[r][:, :, j].bitcast(F32),
                in_=xt_of[r, j][:].rearrange("p g u t -> p g t u"),
            )

        def quantise_x(r):
            x_codes = work.tile([P, X_PASSES, BATCH_TOKENS], U32, align_bytes=64)
            x_scales = work.tile([P, X_PASSES, BATCH_TOKENS], U8, align_bytes=64)
            nc.vector.quantize_mx(
                out=x_codes[:].rearrange("p g t -> p (g t)").bitcast(FP8X4),
                scales=x_scales[:].rearrange("p g t -> p (g t)"),
                in_=x_grouped_of[r][:].rearrange("p g j t s -> p (g j t s)"),
            )
            x_mx_of[r] = (x_codes, x_scales)

        def first_product(r, half):
            x_codes, x_scales = x_mx_of[r]
            h_bank = psum_products.tile([P, 2, BATCH_TOKENS], F32, tag="product")
            for place, f in enumerate(FUNCTION_ORDER[2 * half : 2 * half + 2]):
                for g in range(X_PASSES):
                    nc.tensor.matmul_mx(
                        out=h_bank[:, place, :],
                        lhsT=w_words[:, g, PACK * P * f : PACK * P * (f + 1)].bitcast(FP8X4),
                        lhsT_scale=planes[:, g, P * f : P * (f + 1)],
                        rhs=x_codes[:, g, :].bitcast(FP8X4),
                        rhs_scale=x_scales[:, g, :],
                        start=(g == 0),
                        stop=(g == X_PASSES - 1),
                    )
                h_of[r, f] = h_bank[:, place, :]

        def activate(r):
            h = {f: h_of[r, f] for f in FUNCTION_ORDER}
            c_rows = moved.tile([P, FUNCTIONS, BATCH_TOKENS], BF16)
            half_tanh = work.tile([P, BATCH_TOKENS], F32)
            for f in FUNCTION_ORDER:
                if f == 2:
                    nc.scalar.activation(
                        out=half_tanh[:], in_=h[2], func=ACT.Tanh, bias=half_sigmoid_bias[:, 0:1], scale=0.5
                    )
                    nc.gpsimd.tensor_scalar(
                        out=c_rows[:, 2, :], in0=half_tanh[:], scalar1=0.5, scalar2=0.5, op0=ALU.mult, op1=ALU.add
                    )
                else:
                    nc.scalar.activation(
                        out=c_rows[:, f, :],
                        in_=h[f],
                        func={0: ACT.Relu, 1: ACT.Tanh, 3: ACT.Gelu}[f],
                        bias=bias_columns[:, f : f + 1],
                    )
            c_rows_of[r] = c_rows

        def move_c(r):
            c_rows = c_rows_of[r]
            planar = moved.tile([P, PACK, BATCH_TOKENS], BF16)
            for f in MOVE_ORDER:
                nc.sync.dma_start(
                    out=planar[WORD_ROWS * f : WORD_ROWS * (f + 1), :, :], in_=c_rows[:, f, :]
                )
            planar_of[r] = planar

        def token_pieces(r):
            size = BATCH_TOKENS if r < 3 else P
            return [slice(first, first + size) for first in range(0, BATCH_TOKENS, size)]

        def group_c(r):
            c_grouped = work.tile([P, BATCH_TOKENS, PACK], BF16, align_bytes=64)
            for piece in token_pieces(r):
                nc.vector.tensor_copy(
                    out=c_grouped[:, piece, :].rearrange("p (n i) s -> p n s i", i=4),
                    in_=planar_of[r][:, :, piece].rearrange("p s (n i) -> p n s i", i=4),
                )
            c_grouped_of[r] = c_grouped

        def quantise_c(r):
            c_codes = work.tile([P, BATCH_TOKENS], U32, align_bytes=64)
            c_scales = work.tile([P, BATCH_TOKENS], U8, align_bytes=64)
            for piece in token_pieces(r):
                nc.vector.quantize_mx(
                    out=c_codes[:, piece].bitcast(FP8X4),
                    scales=c_scales[:, piece],
                    in_=c_grouped_of[r][:, piece, :].rearrange("p t s -> p (t s)"),
                )
            c_mx_of[r] = (c_codes, c_scales)

        def second_product(r, j):
            c_codes, c_scales = c_mx_of[r]
            width = D_OUT if r < ROUNDS - 1 else D_OUT // 2
            o_of[r, j] = []
            for first in range(0, D_OUT, width):
                o = psum_products.tile([P, width], F32, tag="product")
                nc.tensor.matmul_mx(
                    out=o[:],
                    lhsT=c_codes[:, P * j : P * (j + 1)].bitcast(FP8X4),
                    lhsT_scale=c_scales[:, P * j : P * (j + 1)],
                    rhs=a_words[:, PACK * first : PACK * (first + width)].bitcast(FP8X4),
                    rhs_scale=planes[:, AGG_PLANE, first : first + width],
                    start=True,
                    stop=True,
                )
                o_of[r, j].append((slice(first, first + width), o))

        def store(r, j):
            if r not in result_of:
                result_of[r] = moved.tile([P, BATCH, D_OUT], F32, name="result")
            result = result_of[r]
            for columns, o in o_of[r, j]:
                on_scalar = (columns.start == 0) == (j == 0) if r == ROUNDS - 1 else (r >= 4 or j == 1)
                copy_out_of_psum(on_scalar, out=result[:, j, columns], in_=o[:])
            if r >= SINGLE_STORES:
                nc.sync.dma_start(out=out_tiles[:, BATCH * r + j, :], in_=result[:, j, :])

        def store_batch(r):
            if r < SINGLE_STORES:
                nc.sync.dma_start(out=out_tiles[:, BATCH * r : BATCH * (r + 1), :], in_=result_of[r][:])

        def in_range(batch):
            return 0 <= batch < ROUNDS

        def step(function, batch, *args):
            if in_range(batch):
                function(batch, *args)

        for r in range(0, ROUNDS + 7):
            if r == 0:
                stage_bias()
            step(quantise_x, r - 1)
            step(transpose_x, r, 0)
            step(store, r - 6, 0)
            step(transpose_x, r, 1)
            step(activate, r - 2)
            step(first_product, r - 1, 0)
            if LOADS_AHEAD <= r + 2 < ROUNDS:
                load_x(r + 2)
            step(store, r - 6, 1)
            if r == 0:
                turn_bias()
            step(group_c, r - 4)
            step(group_x, r, 0)
            step(group_x, r, 1)
            step(first_product, r - 1, 1)
            step(quantise_c, r - 4)
            step(move_c, r - 2)
            step(store_batch, r - 6)
            step(second_product, r - 5, 0)
            step(second_product, r - 5, 1)
